import numpy as np
import ml_dtypes


BF16 = ml_dtypes.bfloat16


def bf(x):
    return np.asarray(x, np.float32).astype(BF16)


def f64(x):
    return np.asarray(x).astype(np.float64)


E2M1 = np.array([0.0, 0.5, 1.0, 1.5, 2.0, 3.0, 4.0, 6.0, -0.0, -0.5, -1.0, -1.5, -2.0, -3.0, -4.0, -6.0])


def pack_weight(w, fmt):
    k, n = w.shape
    w = f64(bf(w)).reshape(k // 32, 32, n)
    amax = np.abs(w).max(1)
    if fmt == "e4m3":
        byte = np.frexp(amax)[1] - 1 + 127 - 7
    else:
        mant, ex = np.frexp(amax / 6.0)
        byte = np.where(mant > 0.5, ex, ex - 1) + 127
    byte = np.clip(np.where(amax > 0, byte, 1), 1, 254)
    scaled = (w * np.exp2(127.0 - byte)[:, None, :]).reshape(k, n).astype(np.float32)
    by_word = np.ascontiguousarray(scaled.reshape(k // 512, 128, 4, n).transpose(0, 1, 3, 2))
    if fmt == "e4m3":
        words = by_word.astype(ml_dtypes.float8_e4m3fn).view(np.uint8)
    else:
        c = by_word.astype(ml_dtypes.float4_e2m1fn).view(np.uint8) & 0xF
        words = c[..., 0::2] | (c[..., 1::2] << 4)
    return np.ascontiguousarray(words), np.ascontiguousarray(byte.astype(np.uint8).reshape(k // 512, 16, n))


def unpack_weight(words, scales, fmt):
    g, p, n, _ = words.shape
    if fmt == "e4m3":
        vals = np.ascontiguousarray(words).view(ml_dtypes.float8_e4m3fn).astype(np.float64)
    else:
        nib = np.empty((g, p, n, 4), np.uint8)
        nib[..., 0::2] = words & 0xF
        nib[..., 1::2] = words >> 4
        vals = E2M1[nib]
    vals = vals * np.repeat(np.exp2(scales.astype(np.float64) - 127.0), 8, axis=1)[..., None]
    return vals.transpose(0, 1, 3, 2).reshape(g * 512, n)

def pack4(w):
    words, scales = pack_weight(w, "e2m1")
    return words.reshape(words.shape[0], 128, -1), scales


def unpack4(words, scales):
    return unpack_weight(words.reshape(words.shape[0], 128, -1, 2), scales, "e2m1")


def kspread(k):
    return np.exp2(np.repeat(np.random.randint(-6, 7, k // 32), 32).astype(np.float64))


B, S, D, E, HD = 2, 512, 1536, 1536, 64
ROPE_BASE = 10000.0


def rope_tables():
    inv_freq = 1.0 / ROPE_BASE ** (np.arange(0, E, 2) / E)
    ang = np.repeat(np.arange(S)[:, None] * inv_freq[None, :], 2, axis=-1)
    return np.cos(ang), np.sin(ang)


def rotate_half(v):
    h = v.shape[-1] // 2
    return np.concatenate([-v[..., h:], v[..., :h]], axis=-1)


def setup_inputs():
    s = kspread(D)
    x = np.random.standard_normal((B, S, D)) * s
    x_words, x_scales = pack4(np.ascontiguousarray(x.reshape(B * S, D).T))
    Wq_words, Wq_scales = pack4(np.random.standard_normal((D, E)) * 0.5 / np.sqrt(D) / s[:, None])
    bq = bf(np.random.standard_normal(E) * 0.1)
    Wk_words, Wk_scales = pack4(np.random.standard_normal((D, E)) * 0.5 / np.sqrt(D) / s[:, None])
    bk = bf(np.random.standard_normal(E) * 0.1)
    return {"x_words": x_words,
            "x_scales": x_scales,
            "Wq_words": Wq_words,
            "Wq_scales": Wq_scales,
            "bq": bq,
            "Wk_words": Wk_words,
            "Wk_scales": Wk_scales,
            "bk": bk}


def reference(x_words, x_scales, Wq_words, Wq_scales, bq, Wk_words, Wk_scales, bk):
    xq = unpack4(x_words, x_scales).T.reshape(B, S, D)
    q = (xq @ unpack4(Wq_words, Wq_scales)) + f64(bq)
    k = (xq @ unpack4(Wk_words, Wk_scales)) + f64(bk)
    cos, sin = rope_tables()
    qr = q * cos + rotate_half(q) * sin
    kr = k * cos + rotate_half(k) * sin
    return qr, kr

@@ -1,0 +1,266 @@
+from contextlib import ExitStack
+import math
+
+import concourse.mybir as mybir
+from concourse.masks import make_identity
+
+F32 = mybir.dt.float32
+BF16 = mybir.dt.bfloat16
+I32 = mybir.dt.int32
+U8 = mybir.dt.uint8
+FP4X4 = mybir.dt.float4_e2m1fn_x4
+ALU = mybir.AluOpType
+ACT = mybir.ActivationFunctionType
+
+NSEQ, S, D, E = 2, 512, 1536, 1536
+ROPE_BASE = 10000.0
+P = 128
+PASSES = D // 512
+HALF = E // 2
+NBLK = E // P
+NPAIR = NBLK // 2
+FREQ_BITS = 10
+FIRST_DIRECT = 7
+PAIR_ORDER = (5, 4, 3, 2, 1, 0)
+FIRST = PAIR_ORDER[0]
+LAG = 2
+FLOPS = 2 * NSEQ * S * D * 2 * E
+
+
+def tile_ropemultiheadattention_pa_kernel(
+    tc, x_words, x_scales, Wq_words, Wq_scales, bq, Wk_words, Wk_scales, bk, out_0, out_1
+):
+    nc = tc.nc
+    w_words = (Wq_words, Wk_words)
+    w_scales = (Wq_scales, Wk_scales)
+    biases = (bq, bk)
+    outs = (out_0, out_1)
+
+    with ExitStack() as ctx:
+        keep = ctx.enter_context(tc.tile_pool(name="keep", bufs=1))
+        work = ctx.enter_context(tc.tile_pool(name="work", bufs=2))
+        psum_acc = ctx.enter_context(tc.psum_pool(name="psum_acc", bufs=4))
+        psum_tr = ctx.enter_context(tc.psum_pool(name="psum_tr", bufs=4))
+        ctx.enter_context(tc.manual_schedule())
+
+        xw = [keep.tile([P, PASSES, 2 * S], U8, name="xw%d" % b, align_bytes=64) for b in range(NSEQ)]
+        xs = [keep.tile([P, PASSES, S], U8, name="xs%d" % b, align_bytes=64) for b in range(NSEQ)]
+        ws = [keep.tile([P, PASSES, E], U8, name="ws%d" % m, align_bytes=64) for m in range(2)]
+        wc_first = [keep.tile([P, PASSES, 2, 2 * P], U8, name="wcf%d" % m, align_bytes=64) for m in range(2)]
+        wc_rest = [
+            keep.tile([P, PASSES, 2, 2 * P * FIRST], U8, name="wcr%d" % m, align_bytes=64) for m in range(2)
+        ]
+
+        def flat(t):
+            return t[:].rearrange("p g n -> p (g n)")
+
+        def load_codes(dst, words, first_byte):
+            nbytes = dst.shape[2]
+            nc.sync.dma_start(
+                out=dst.bitcast(I32),
+                in_=words[:, :, first_byte : first_byte + nbytes].rearrange("g p n -> p g n").bitcast(I32),
+            )
+
+        def load_planes(dst, scales, first_col):
+            ncols = dst.shape[2]
+            for q in range(4):
+                nc.sync.dma_start(
+                    out=dst[32 * q : 32 * q + 4, :, :].bitcast(I32),
+                    in_=scales[:, 4 * q : 4 * q + 4, first_col : first_col + ncols]
+                    .rearrange("g r n -> r g n")
+                    .bitcast(I32),
+                )
+
+        warm = keep.tile([P, 1], F32, name="warm")
+        warm_out = keep.tile([P, 1], F32, name="warm_out")
+        brows = keep.tile([P, P], BF16, name="brows")
+        nc.vector.memset(warm[:], 0.0)
+        nc.vector.memset(brows[:], 0.0)
+        nc.vector.memset(flat(xs[0]).bitcast(I32), 0)
+        nc.vector.memset(flat(ws[0]).bitcast(I32), 0)
+
+        for m in range(2):
+            rows = biases[m].rearrange("(c p) -> c p", p=P)
+            nc.scalar.dma_start(out=brows[NBLK * m : NBLK * m + 8, :], in_=rows[0:8, :])
+            nc.scalar.dma_start(out=brows[NBLK * m + 8 : NBLK * m + 12, :], in_=rows[8:12, :])
+        nc.scalar.activation(out=warm_out[:], in_=warm[:], func=ACT.Sin)
+
+        idx = keep.tile([P, NBLK], I32, name="idx")
+        nc.gpsimd.iota(idx[:], pattern=[[-P, NBLK]], base=2 ** (FREQ_BITS + 1) - 1, channel_multiplier=-1)
+        ident = keep.tile([P, P], F32, name="ident")
+        make_identity(nc, ident[:])
+        pos = keep.tile([P, S], F32, name="pos")
+        nc.gpsimd.iota(pos[:], pattern=[[1, S]], base=0, channel_multiplier=0, allow_small_or_imprecise_dtypes=True)
+        nc.gpsimd.memset(flat(xs[1]).bitcast(F32), 0.0)
+        nc.gpsimd.memset(flat(ws[1]).bitcast(F32), 0.0)
+
+        load_planes(xs[0], x_scales, 0)
+        load_planes(ws[0], w_scales[0], 0)
+        load_codes(xw[0][:, :, :], x_words, 0)
+        for h in (1, 0):
+            load_codes(wc_first[0][:, :, h, :], w_words[0], 2 * P * (FIRST + NPAIR * h))
+        load_planes(xs[1], x_scales, S)
+        load_codes(xw[1][:, :, :], x_words, 2 * S)
+        load_planes(ws[1], w_scales[1], 0)
+        for h in (1, 0):
+            load_codes(wc_first[1][:, :, h, :], w_words[1], 2 * P * (FIRST + NPAIR * h))
+        for m in range(2):
+            for h in (1, 0):
+                load_codes(wc_rest[m][:, :, h, :], w_words[m], 2 * HALF * h)
+
+        one = keep.tile([P, 1], F32, name="one")
+        halfpi = keep.tile([P, 1], F32, name="halfpi")
+        nc.vector.memset(one[:], 1.0)
+        nc.vector.tensor_scalar(out=halfpi[:], in0=one[:], scalar1=math.pi / 2, scalar2=None, op0=ALU.mult)
+        bit = keep.tile([P, FREQ_BITS, NBLK], I32, name="bit")
+        fac = keep.tile([P, FREQ_BITS, NBLK], F32, name="fac")
+        for k in range(FREQ_BITS):
+            nc.vector.tensor_scalar(
+                out=bit[:, k, :], in0=idx[:], scalar1=k + 1, scalar2=1,
+                op0=ALU.logical_shift_right, op1=ALU.bitwise_and,
+            )
+        for k in range(FREQ_BITS):
+            nc.vector.tensor_scalar(
+                out=fac[:, k, :], in0=bit[:, k, :], scalar1=ROPE_BASE ** ((2.0 ** k) / HALF) - 1.0, scalar2=1.0,
+                op0=ALU.mult, op1=ALU.add,
+            )
+        p5 = keep.tile([P, 5, NBLK], F32, name="p5")
+        p2 = keep.tile([P, 2, NBLK], F32, name="p2")
+        p1 = keep.tile([P, NBLK], F32, name="p1")
+        frad = keep.tile([P, NBLK], F32, name="frad")
+        nfrad = keep.tile([P, NBLK], F32, name="nfrad")
+        turn = keep.tile([P, NBLK], F32, name="turn")
+        nc.vector.tensor_tensor(out=p5[:], in0=fac[:, 0:5, :], in1=fac[:, 5:10, :], op=ALU.mult)
+        nc.vector.tensor_tensor(out=p2[:], in0=p5[:, 0:2, :], in1=p5[:, 2:4, :], op=ALU.mult)
+        nc.vector.tensor_tensor(out=p1[:], in0=p2[:, 0, :], in1=p2[:, 1, :], op=ALU.mult)
+        nc.vector.scalar_tensor_tensor(
+            out=frad[:], in0=p1[:], scalar=ROPE_BASE ** (-(2.0 ** FREQ_BITS - 1.0) / HALF), in1=p5[:, 4, :],
+            op0=ALU.mult, op1=ALU.mult,
+        )
+        nc.vector.tensor_scalar(out=turn[:], in0=frad[:], scalar1=0.5 / math.pi, scalar2=None, op0=ALU.mult)
+        nc.vector.tensor_scalar(out=nfrad[:], in0=frad[:], scalar1=-1.0, scalar2=None, op0=ALU.mult)
+
+        brows32 = keep.tile([P, P], F32, name="brows32")
+        nc.scalar.copy(out=brows32[:], in_=brows[:])
+        bias_ps = psum_tr.tile([P, S], F32, name="tr")
+        nc.tensor.transpose(out=bias_ps[:, 0:P], in_=brows32[:], identity=ident[:])
+        bias = keep.tile([P, 2 * NBLK], F32, name="bias")
+        nc.scalar.copy(out=bias[:], in_=bias_ps[:, 0 : 2 * NBLK])
+
+        cos = [keep.tile([P, S], F32, name="cos%d" % c) for c in range(NBLK)]
+        sin = [keep.tile([P, S], F32, name="sin%d" % c) for c in range(NBLK)]
+        frac = {}
+        absfrac = {}
+
+        def reduce_angle(c):
+            n = work.tile([P, S], I32, name="turns")
+            nc.vector.tensor_scalar(out=n[:], in0=pos[:], scalar1=turn[:, c : c + 1], scalar2=None, op0=ALU.mult)
+            r = work.tile([P, S], F32, name="frac")
+            nc.vector.scalar_tensor_tensor(
+                out=r[:], in0=pos[:], scalar=turn[:, c : c + 1], in1=n[:], op0=ALU.mult, op1=ALU.subtract
+            )
+            frac[c] = r
+
+        def table_step(kind, c):
+            if kind == "direct_cos":
+                nc.scalar.activation(
+                    out=cos[c][:], in_=pos[:], func=ACT.Sin, scale=nfrad[:, c : c + 1], bias=halfpi[:, 0:1]
+                )
+            elif kind == "direct_sin":
+                nc.scalar.activation(out=sin[c][:], in_=pos[:], func=ACT.Sin, scale=frad[:, c : c + 1])
+            elif kind == "abs":
+                a = work.tile([P, S], F32, name="absfrac")
+                nc.scalar.activation(out=a[:], in_=frac[c][:], func=ACT.Abs)
+                absfrac[c] = a
+            elif kind == "cos":
+                nc.scalar.activation(
+                    out=cos[c][:], in_=absfrac[c][:], func=ACT.Sin, scale=-2.0 * math.pi, bias=halfpi[:, 0:1]
+                )
+            else:
+                sign = -1.0 if c < NPAIR else 1.0
+                nc.scalar.activation(out=sin[c][:], in_=frac[c][:], func=ACT.Sin, scale=sign * 2.0 * math.pi)
+
+        def prepare_tables(c):
+            steps = []
+            for blk in (c + NPAIR, c):
+                if blk >= FIRST_DIRECT:
+                    steps.extend([("direct_cos", blk), ("direct_sin", blk)])
+                else:
+                    reduce_angle(blk)
+                    steps.extend([("abs", blk), ("cos", blk), ("sin", blk)])
+            return steps
+
+        units = [(m, c, b) for c in PAIR_ORDER for m in range(2) for b in range(NSEQ)]
+
+        def w_codes(m, c, h, g):
+            if c == FIRST:
+                return wc_first[m][:, g, h, :]
+            return wc_rest[m][:, g, h, 2 * P * c : 2 * P * (c + 1)]
+
+        def project(u):
+            m, c, b = units[u]
+            acc = {}
+            for h in (1, 0):
+                blk = c + NPAIR * h
+                acc[h] = psum_acc.tile([P, S], F32, name="acc")
+                for g in range(PASSES):
+                    nc.tensor.matmul_mx(
+                        out=acc[h][:],
+                        lhsT=w_codes(m, c, h, g).bitcast(FP4X4),
+                        lhsT_scale=ws[m][:, g, P * blk : P * (blk + 1)],
+                        rhs=xw[b][:, g, :].bitcast(FP4X4),
+                        rhs_scale=xs[b][:, g, :],
+                        start=(g == 0),
+                        stop=(g == PASSES - 1),
+                    )
+            return acc
+
+        def rotate(u, acc):
+            m, c, b = units[u]
+            bcol = {h: bias[:, NBLK * m + c + NPAIR * h : NBLK * m + c + NPAIR * h + 1] for h in (0, 1)}
+            o = {}
+            for h in (1, 0):
+                blk = c + NPAIR * h
+                t1 = work.tile([P, S], F32, name="t1", bufs=4)
+                t2 = work.tile([P, S], F32, name="t2", bufs=4)
+                nc.vector.scalar_tensor_tensor(
+                    out=t1[:], in0=acc[h][:], scalar=bcol[h], in1=cos[blk][:], op0=ALU.add, op1=ALU.mult
+                )
+                nc.vector.scalar_tensor_tensor(
+                    out=t2[:], in0=acc[1 - h][:], scalar=bcol[1 - h], in1=sin[blk][:], op0=ALU.add, op1=ALU.mult
+                )
+                o[h] = work.tile([P, S], F32, name="o", bufs=8)
+                nc.gpsimd.tensor_tensor(out=o[h][:], in0=t1[:], in1=t2[:], op=ALU.add)
+            return o
+
+        def emit(u, o):
+            m, c, b = units[u]
+            rows = outs[m][b].rearrange("(t p) e -> p t e", p=P)
+            tr = {}
+            for h in (1, 0):
+                tr[h] = psum_tr.tile([P, S], F32, name="tr")
+                for t in range(S // P):
+                    nc.tensor.transpose(
+                        out=tr[h][:, P * t : P * (t + 1)], in_=o[h][:, P * t : P * (t + 1)], identity=ident[:]
+                    )
+            for h in (1, 0):
+                blk = c + NPAIR * h
+                st = work.tile([P, S // P, P], F32, name="st", bufs=6)
+                nc.scalar.copy(out=st[:].rearrange("p t e -> p (t e)"), in_=tr[h][:])
+                nc.sync.dma_start(out=rows[:, :, P * blk : P * (blk + 1)], in_=st[:])
+
+        for kind, c in prepare_tables(FIRST):
+            table_step(kind, c)
+
+        pending = []
+        rotated = {}
+        for s in range(len(units) + LAG):
+            if s < len(units):
+                rotated[s] = rotate(s, project(s))
+                if s % 4 == 0 and s // 4 + 1 < NPAIR:
+                    pending = pending + prepare_tables(PAIR_ORDER[s // 4 + 1])
+            if s >= LAG:
+                emit(s - LAG, rotated[s - LAG])
+            for kind, c in pending[:2]:
+                table_step(kind, c)
+            pending = pending[2:]

@@ -7,6 +7,7 @@ from concourse.masks import make_identity
 F32 = mybir.dt.float32
 BF16 = mybir.dt.bfloat16
 I32 = mybir.dt.int32
+U32 = mybir.dt.uint32
 U8 = mybir.dt.uint8
 FP4X4 = mybir.dt.float4_e2m1fn_x4
 ALU = mybir.AluOpType
@@ -19,11 +20,13 @@ PASSES = D // 512
 HALF = E // 2
 NBLK = E // P
 NPAIR = NBLK // 2
+NT = S // P
 FREQ_BITS = 10
+FOLDED = 6
 FIRST_DIRECT = 7
 PAIR_ORDER = (5, 4, 3, 2, 1, 0)
 FIRST = PAIR_ORDER[0]
-LAG = 2
+V_ADD_UNITS = ()
 FLOPS = 2 * NSEQ * S * D * 2 * E
 
 
@@ -71,11 +74,15 @@ def tile_ropemultiheadattention_pa_kernel(
                     .bitcast(I32),
                 )
 
+        def load_first_codes(m):
+            for h in (1, 0):
+                load_codes(wc_first[m][:, :, h, :], w_words[m], 2 * P * (FIRST + NPAIR * h))
+
         warm = keep.tile([P, 1], F32, name="warm")
         warm_out = keep.tile([P, 1], F32, name="warm_out")
         brows = keep.tile([P, P], BF16, name="brows")
-        nc.vector.memset(warm[:], 0.0)
         nc.vector.memset(brows[:], 0.0)
+        nc.vector.memset(warm[:], 0.0)
         nc.vector.memset(flat(xs[0]).bitcast(I32), 0)
         nc.vector.memset(flat(ws[0]).bitcast(I32), 0)
 
@@ -94,24 +101,24 @@ def tile_ropemultiheadattention_pa_kernel(
         nc.gpsimd.memset(flat(xs[1]).bitcast(F32), 0.0)
         nc.gpsimd.memset(flat(ws[1]).bitcast(F32), 0.0)
 
+        load_codes(xw[0][:, :, :], x_words, 0)
+        load_first_codes(0)
         load_planes(xs[0], x_scales, 0)
         load_planes(ws[0], w_scales[0], 0)
-        load_codes(xw[0][:, :, :], x_words, 0)
-        for h in (1, 0):
-            load_codes(wc_first[0][:, :, h, :], w_words[0], 2 * P * (FIRST + NPAIR * h))
         load_planes(xs[1], x_scales, S)
         load_codes(xw[1][:, :, :], x_words, 2 * S)
         load_planes(ws[1], w_scales[1], 0)
-        for h in (1, 0):
-            load_codes(wc_first[1][:, :, h, :], w_words[1], 2 * P * (FIRST + NPAIR * h))
+        load_first_codes(1)
         for m in range(2):
             for h in (1, 0):
                 load_codes(wc_rest[m][:, :, h, :], w_words[m], 2 * HALF * h)
 
         one = keep.tile([P, 1], F32, name="one")
-        halfpi = keep.tile([P, 1], F32, name="halfpi")
+        angle = {}
         nc.vector.memset(one[:], 1.0)
-        nc.vector.tensor_scalar(out=halfpi[:], in0=one[:], scalar1=math.pi / 2, scalar2=None, op0=ALU.mult)
+        for name, value in (("halfpi", math.pi / 2), ("neghalfpi", -math.pi / 2), ("negpi", -math.pi)):
+            angle[name] = keep.tile([P, 1], F32, name=name)
+            nc.vector.tensor_scalar(out=angle[name][:], in0=one[:], scalar1=value, scalar2=None, op0=ALU.mult)
         bit = keep.tile([P, FREQ_BITS, NBLK], I32, name="bit")
         fac = keep.tile([P, FREQ_BITS, NBLK], F32, name="fac")
         for k in range(FREQ_BITS):
@@ -149,48 +156,59 @@ def tile_ropemultiheadattention_pa_kernel(
 
         cos = [keep.tile([P, S], F32, name="cos%d" % c) for c in range(NBLK)]
         sin = [keep.tile([P, S], F32, name="sin%d" % c) for c in range(NBLK)]
-        frac = {}
-        absfrac = {}
+        scratch = {}
 
-        def reduce_angle(c):
-            n = work.tile([P, S], I32, name="turns")
-            nc.vector.tensor_scalar(out=n[:], in0=pos[:], scalar1=turn[:, c : c + 1], scalar2=None, op0=ALU.mult)
-            r = work.tile([P, S], F32, name="frac")
-            nc.vector.scalar_tensor_tensor(
-                out=r[:], in0=pos[:], scalar=turn[:, c : c + 1], in1=n[:], op0=ALU.mult, op1=ALU.subtract
-            )
-            frac[c] = r
+        def col(t, c):
+            return t[:, c : c + 1]
+
+        def sine(out, in_, scale, bias_name=None):
+            if bias_name is None:
+                nc.scalar.activation(out=out[:], in_=in_[:], func=ACT.Sin, scale=scale)
+            else:
+                nc.scalar.activation(out=out[:], in_=in_[:], func=ACT.Sin, scale=scale, bias=angle[bias_name][:])
 
         def table_step(kind, c):
             if kind == "direct_cos":
-                nc.scalar.activation(
-                    out=cos[c][:], in_=pos[:], func=ACT.Sin, scale=nfrad[:, c : c + 1], bias=halfpi[:, 0:1]
-                )
+                sine(cos[c], pos, col(nfrad, c), "halfpi")
             elif kind == "direct_sin":
-                nc.scalar.activation(out=sin[c][:], in_=pos[:], func=ACT.Sin, scale=frad[:, c : c + 1])
-            elif kind == "abs":
+                sine(sin[c], pos, col(frad, c))
+            elif kind == "fold_cos":
                 a = work.tile([P, S], F32, name="absfrac")
-                nc.scalar.activation(out=a[:], in_=frac[c][:], func=ACT.Abs)
-                absfrac[c] = a
-            elif kind == "cos":
+                nc.scalar.activation(out=a[:], in_=pos[:], func=ACT.Abs, scale=col(frad, c), bias=angle["negpi"][:])
+                sine(cos[c], a, 1.0, "neghalfpi")
+            elif kind == "fold_sin":
+                a = work.tile([P, S], F32, name="absfrac")
                 nc.scalar.activation(
-                    out=cos[c][:], in_=absfrac[c][:], func=ACT.Sin, scale=-2.0 * math.pi, bias=halfpi[:, 0:1]
+                    out=a[:], in_=pos[:], func=ACT.Abs, scale=col(frad, c), bias=angle["neghalfpi"][:]
                 )
+                sine(sin[c], a, -1.0, "halfpi")
+            elif kind == "turns":
+                n = work.tile([P, S], U32, name="turns")
+                nc.scalar.activation(out=n[:], in_=pos[:], func=ACT.Copy, scale=col(turn, c))
+                scratch["n", c] = n[:].bitcast(I32)
+            elif kind == "frac":
+                r = work.tile([P, S], F32, name="frac")
+                nc.vector.scalar_tensor_tensor(
+                    out=r[:], in0=pos[:], scalar=col(turn, c), in1=scratch["n", c], op0=ALU.mult, op1=ALU.subtract
+                )
+                scratch["r", c] = r
+            elif kind == "cos":
+                a = work.tile([P, S], F32, name="absfrac")
+                nc.scalar.activation(out=a[:], in_=scratch["r", c][:], func=ACT.Abs)
+                sine(cos[c], a, -2.0 * math.pi, "halfpi")
             else:
-                sign = -1.0 if c < NPAIR else 1.0
-                nc.scalar.activation(out=sin[c][:], in_=frac[c][:], func=ACT.Sin, scale=sign * 2.0 * math.pi)
+                sine(sin[c], scratch["r", c], -2.0 * math.pi)
 
-        def prepare_tables(c):
-            steps = []
-            for blk in (c + NPAIR, c):
-                if blk >= FIRST_DIRECT:
-                    steps.extend([("direct_cos", blk), ("direct_sin", blk)])
-                else:
-                    reduce_angle(blk)
-                    steps.extend([("abs", blk), ("cos", blk), ("sin", blk)])
-            return steps
+        def table_plan(c):
+            hi = c + NPAIR
+            if hi >= FIRST_DIRECT:
+                upper = [("direct_cos", hi), ("direct_sin", hi)]
+            else:
+                upper = [("fold_cos", hi), ("fold_sin", hi)]
+            return [("turns", c)] + upper, [("frac", c)], [("cos", c), ("sin", c)]
 
         units = [(m, c, b) for c in PAIR_ORDER for m in range(2) for b in range(NSEQ)]
+        last = len(units) - 1
 
         def w_codes(m, c, h, g):
             if c == FIRST:
@@ -215,52 +233,100 @@ def tile_ropemultiheadattention_pa_kernel(
                     )
             return acc
 
-        def rotate(u, acc):
+        def products(u, acc, h, t1, t2):
             m, c, b = units[u]
-            bcol = {h: bias[:, NBLK * m + c + NPAIR * h : NBLK * m + c + NPAIR * h + 1] for h in (0, 1)}
-            o = {}
-            for h in (1, 0):
-                blk = c + NPAIR * h
-                t1 = work.tile([P, S], F32, name="t1", bufs=4)
-                t2 = work.tile([P, S], F32, name="t2", bufs=4)
-                nc.vector.scalar_tensor_tensor(
-                    out=t1[:], in0=acc[h][:], scalar=bcol[h], in1=cos[blk][:], op0=ALU.add, op1=ALU.mult
-                )
-                nc.vector.scalar_tensor_tensor(
-                    out=t2[:], in0=acc[1 - h][:], scalar=bcol[1 - h], in1=sin[blk][:], op0=ALU.add, op1=ALU.mult
-                )
-                o[h] = work.tile([P, S], F32, name="o", bufs=8)
-                nc.gpsimd.tensor_tensor(out=o[h][:], in0=t1[:], in1=t2[:], op=ALU.add)
-            return o
+            blk = c + NPAIR * h
+            own = col(bias, NBLK * m + blk)
+            other = col(bias, NBLK * m + c + NPAIR * (1 - h))
+            nc.vector.scalar_tensor_tensor(
+                out=t1, in0=acc[h][:], scalar=own, in1=cos[blk][:], op0=ALU.add, op1=ALU.mult
+            )
+            nc.vector.scalar_tensor_tensor(
+                out=t2, in0=acc[1 - h][:], scalar=other, in1=sin[blk][:], op0=ALU.add, op1=ALU.mult
+            )
 
-        def emit(u, o):
+        def rotate(u, acc):
+            if u == last or u in V_ADD_UNITS:
+                out = {}
+                for h in (1, 0):
+                    t1 = work.tile([P, S], F32, name="t1h", bufs=2)
+                    t2 = work.tile([P, S], F32, name="t2h", bufs=2)
+                    oh = work.tile([P, S], F32, name="oh", bufs=4)
+                    products(u, acc, h, t1[:], t2[:])
+                    engine = nc.gpsimd if h == 1 else nc.vector
+                    engine.tensor_tensor(out=oh[:], in0=t1[:], in1=t2[:], op=ALU.add)
+                    out[h] = oh[:]
+                return out
+            t1 = work.tile([P, 2, S], F32, name="t1", bufs=3)
+            t2 = work.tile([P, 2, S], F32, name="t2", bufs=3)
+            o = work.tile([P, 2, S], F32, name="o", bufs=6)
+            for h in (1, 0):
+                products(u, acc, h, t1[:, h, :], t2[:, h, :])
+            nc.gpsimd.tensor_tensor(out=o[:], in0=t1[:], in1=t2[:], op=ALU.add)
+            return {h: o[:, h, :] for h in (0, 1)}
+
+        def store(u, h, t0, st):
             m, c, b = units[u]
+            blk = c + NPAIR * h
             rows = outs[m][b].rearrange("(t p) e -> p t e", p=P)
+            nc.sync.dma_start(out=rows[:, t0 : t0 + st.shape[1], P * blk : P * (blk + 1)], in_=st[:])
+
+        def emit(batch):
+            tr = {}
+            for u in batch:
+                for h in (1, 0):
+                    tr[u, h] = psum_tr.tile([P, S], F32, name="tr")
+                    for t in range(NT):
+                        nc.tensor.transpose(
+                            out=tr[u, h][:, P * t : P * (t + 1)],
+                            in_=rotated[u][h][:, P * t : P * (t + 1)],
+                            identity=ident[:],
+                        )
+            for u in batch:
+                for h in (1, 0):
+                    st = work.tile([P, NT, P], F32, name="st", bufs=8)
+                    nc.scalar.copy(out=st[:].rearrange("p t e -> p (t e)"), in_=tr[u, h][:])
+                    store(u, h, 0, st)
+
+        def emit_last(u):
             tr = {}
             for h in (1, 0):
-                tr[h] = psum_tr.tile([P, S], F32, name="tr")
-                for t in range(S // P):
-                    nc.tensor.transpose(
-                        out=tr[h][:, P * t : P * (t + 1)], in_=o[h][:, P * t : P * (t + 1)], identity=ident[:]
-                    )
+                for j in range(2):
+                    tr[h, j] = psum_tr.tile([P, S], F32, name="tr")
+                    for t in range(2):
+                        nc.tensor.transpose(
+                            out=tr[h, j][:, P * t : P * (t + 1)],
+                            in_=rotated[u][h][:, P * (2 * j + t) : P * (2 * j + t + 1)],
+                            identity=ident[:],
+                        )
             for h in (1, 0):
-                blk = c + NPAIR * h
-                st = work.tile([P, S // P, P], F32, name="st", bufs=6)
-                nc.scalar.copy(out=st[:].rearrange("p t e -> p (t e)"), in_=tr[h][:])
-                nc.sync.dma_start(out=rows[:, :, P * blk : P * (blk + 1)], in_=st[:])
+                for j in range(2):
+                    st = work.tile([P, 2, P], F32, name="st2", bufs=4)
+                    flat_st = st[:].rearrange("p t e -> p (t e)")
+                    if h == 0 and j == 1:
+                        nc.vector.tensor_copy(out=flat_st, in_=tr[h, j][:, 0 : 2 * P])
+                    else:
+                        nc.scalar.copy(out=flat_st, in_=tr[h, j][:, 0 : 2 * P])
+                    store(u, h, 2 * j, st)
 
-        for kind, c in prepare_tables(FIRST):
-            table_step(kind, c)
-
-        pending = []
-        rotated = {}
-        for s in range(len(units) + LAG):
-            if s < len(units):
-                rotated[s] = rotate(s, project(s))
-                if s % 4 == 0 and s // 4 + 1 < NPAIR:
-                    pending = pending + prepare_tables(PAIR_ORDER[s // 4 + 1])
-            if s >= LAG:
-                emit(s - LAG, rotated[s - LAG])
-            for kind, c in pending[:2]:
+        for stretch in table_plan(FIRST):
+            for kind, c in stretch:
                 table_step(kind, c)
-            pending = pending[2:]
+
+        rotated = {}
+        for k in range(len(units) // 2):
+            plan = None
+            if k % 2 == 0 and k // 2 + 1 < NPAIR:
+                plan = table_plan(PAIR_ORDER[k // 2 + 1])
+                held = plan
+            rotated[2 * k] = rotate(2 * k, project(2 * k))
+            if k % 2 == 1 and k // 2 + 1 < NPAIR:
+                for kind, c in held[1] + held[2]:
+                    table_step(kind, c)
+            rotated[2 * k + 1] = rotate(2 * k + 1, project(2 * k + 1))
+            emit([u for u in (2 * k - 3, 2 * k - 2) if u >= 0])
+            if k % 2 == 0 and k // 2 + 1 < NPAIR:
+                for kind, c in held[0]:
+                    table_step(kind, c)
+        emit([last - 2, last - 1])
+        emit_last(last)

@@ -21,12 +21,13 @@ HALF = E // 2
 NBLK = E // P
 NPAIR = NBLK // 2
 NT = S // P
+BIAS_ROW = 3 * P
 FREQ_BITS = 10
-FOLDED = 6
 FIRST_DIRECT = 7
 PAIR_ORDER = (5, 4, 3, 2, 1, 0)
 FIRST = PAIR_ORDER[0]
-V_ADD_UNITS = ()
+NARROW_UNITS = (20, 21)
+ACC_UNITS = (22, 23)
 FLOPS = 2 * NSEQ * S * D * 2 * E
 
 
@@ -80,16 +81,14 @@ def tile_ropemultiheadattention_pa_kernel(
 
         warm = keep.tile([P, 1], F32, name="warm")
         warm_out = keep.tile([P, 1], F32, name="warm_out")
-        brows = keep.tile([P, P], BF16, name="brows")
+        brows = keep.tile([P, BIAS_ROW], BF16, name="brows")
         nc.vector.memset(brows[:], 0.0)
         nc.vector.memset(warm[:], 0.0)
         nc.vector.memset(flat(xs[0]).bitcast(I32), 0)
         nc.vector.memset(flat(ws[0]).bitcast(I32), 0)
 
         for m in range(2):
-            rows = biases[m].rearrange("(c p) -> c p", p=P)
-            nc.scalar.dma_start(out=brows[NBLK * m : NBLK * m + 8, :], in_=rows[0:8, :])
-            nc.scalar.dma_start(out=brows[NBLK * m + 8 : NBLK * m + 12, :], in_=rows[8:12, :])
+            nc.scalar.dma_start(out=brows[4 * m : 4 * m + 4, :], in_=biases[m].rearrange("(r n) -> r n", n=BIAS_ROW))
         nc.scalar.activation(out=warm_out[:], in_=warm[:], func=ACT.Sin)
 
         idx = keep.tile([P, NBLK], I32, name="idx")
@@ -113,12 +112,21 @@ def tile_ropemultiheadattention_pa_kernel(
             for h in (1, 0):
                 load_codes(wc_rest[m][:, :, h, :], w_words[m], 2 * HALF * h)
 
+        brows32 = keep.tile([P, BIAS_ROW], F32, name="brows32")
+        nc.scalar.copy(out=brows32[:], in_=brows[:])
+        bias_ps = psum_tr.tile([P, S], F32, name="tr")
+        for j in range(3):
+            nc.tensor.transpose(
+                out=bias_ps[:, P * j : P * (j + 1)], in_=brows32[:, P * j : P * (j + 1)], identity=ident[:]
+            )
+        bias = keep.tile([P, 3, 8], F32, name="bias")
+        nc.scalar.copy(out=bias[:], in_=bias_ps[:, 0:BIAS_ROW].rearrange("p (j r) -> p j r", j=3)[:, :, 0:8])
+
+        def bias_col(m, blk):
+            return bias[:, blk % 3, 4 * m + blk // 3 : 4 * m + blk // 3 + 1]
+
         one = keep.tile([P, 1], F32, name="one")
-        angle = {}
         nc.vector.memset(one[:], 1.0)
-        for name, value in (("halfpi", math.pi / 2), ("neghalfpi", -math.pi / 2), ("negpi", -math.pi)):
-            angle[name] = keep.tile([P, 1], F32, name=name)
-            nc.vector.tensor_scalar(out=angle[name][:], in0=one[:], scalar1=value, scalar2=None, op0=ALU.mult)
         bit = keep.tile([P, FREQ_BITS, NBLK], I32, name="bit")
         fac = keep.tile([P, FREQ_BITS, NBLK], F32, name="fac")
         for k in range(FREQ_BITS):
@@ -131,32 +139,29 @@ def tile_ropemultiheadattention_pa_kernel(
                 out=fac[:, k, :], in0=bit[:, k, :], scalar1=ROPE_BASE ** ((2.0 ** k) / HALF) - 1.0, scalar2=1.0,
                 op0=ALU.mult, op1=ALU.add,
             )
+        angle = {}
+        for name, value in (("halfpi", math.pi / 2), ("neghalfpi", -math.pi / 2), ("negpi", -math.pi)):
+            angle[name] = keep.tile([P, 1], F32, name=name)
+            nc.vector.tensor_scalar(out=angle[name][:], in0=one[:], scalar1=value, scalar2=None, op0=ALU.mult)
         p5 = keep.tile([P, 5, NBLK], F32, name="p5")
         p2 = keep.tile([P, 2, NBLK], F32, name="p2")
         p1 = keep.tile([P, NBLK], F32, name="p1")
-        frad = keep.tile([P, NBLK], F32, name="frad")
-        nfrad = keep.tile([P, NBLK], F32, name="nfrad")
-        turn = keep.tile([P, NBLK], F32, name="turn")
         nc.vector.tensor_tensor(out=p5[:], in0=fac[:, 0:5, :], in1=fac[:, 5:10, :], op=ALU.mult)
         nc.vector.tensor_tensor(out=p2[:], in0=p5[:, 0:2, :], in1=p5[:, 2:4, :], op=ALU.mult)
         nc.vector.tensor_tensor(out=p1[:], in0=p2[:, 0, :], in1=p2[:, 1, :], op=ALU.mult)
-        nc.vector.scalar_tensor_tensor(
-            out=frad[:], in0=p1[:], scalar=ROPE_BASE ** (-(2.0 ** FREQ_BITS - 1.0) / HALF), in1=p5[:, 4, :],
-            op0=ALU.mult, op1=ALU.mult,
-        )
-        nc.vector.tensor_scalar(out=turn[:], in0=frad[:], scalar1=0.5 / math.pi, scalar2=None, op0=ALU.mult)
-        nc.vector.tensor_scalar(out=nfrad[:], in0=frad[:], scalar1=-1.0, scalar2=None, op0=ALU.mult)
-
-        brows32 = keep.tile([P, P], F32, name="brows32")
-        nc.scalar.copy(out=brows32[:], in_=brows[:])
-        bias_ps = psum_tr.tile([P, S], F32, name="tr")
-        nc.tensor.transpose(out=bias_ps[:, 0:P], in_=brows32[:], identity=ident[:])
-        bias = keep.tile([P, 2 * NBLK], F32, name="bias")
-        nc.scalar.copy(out=bias[:], in_=bias_ps[:, 0 : 2 * NBLK])
+        lowest = ROPE_BASE ** (-(2.0 ** FREQ_BITS - 1.0) / HALF)
+        turn = keep.tile([P, NBLK], F32, name="turn")
+        frad = keep.tile([P, NBLK], F32, name="frad")
+        nfrad = keep.tile([P, NBLK], F32, name="nfrad")
+        for t, factor in ((turn, lowest * 0.5 / math.pi), (frad, lowest), (nfrad, -lowest)):
+            nc.vector.scalar_tensor_tensor(
+                out=t[:], in0=p1[:], scalar=factor, in1=p5[:, 4, :], op0=ALU.mult, op1=ALU.mult
+            )
 
         cos = [keep.tile([P, S], F32, name="cos%d" % c) for c in range(NBLK)]
         sin = [keep.tile([P, S], F32, name="sin%d" % c) for c in range(NBLK)]
-        scratch = {}
+        turns = {}
+        frac = {}
 
         def col(t, c):
             return t[:, c : c + 1]
@@ -167,45 +172,47 @@ def tile_ropemultiheadattention_pa_kernel(
             else:
                 nc.scalar.activation(out=out[:], in_=in_[:], func=ACT.Sin, scale=scale, bias=angle[bias_name][:])
 
-        def table_step(kind, c):
-            if kind == "direct_cos":
-                sine(cos[c], pos, col(nfrad, c), "halfpi")
-            elif kind == "direct_sin":
-                sine(sin[c], pos, col(frad, c))
-            elif kind == "fold_cos":
-                a = work.tile([P, S], F32, name="absfrac")
-                nc.scalar.activation(out=a[:], in_=pos[:], func=ACT.Abs, scale=col(frad, c), bias=angle["negpi"][:])
-                sine(cos[c], a, 1.0, "neghalfpi")
-            elif kind == "fold_sin":
-                a = work.tile([P, S], F32, name="absfrac")
-                nc.scalar.activation(
-                    out=a[:], in_=pos[:], func=ACT.Abs, scale=col(frad, c), bias=angle["neghalfpi"][:]
-                )
-                sine(sin[c], a, -1.0, "halfpi")
-            elif kind == "turns":
-                n = work.tile([P, S], U32, name="turns")
-                nc.scalar.activation(out=n[:], in_=pos[:], func=ACT.Copy, scale=col(turn, c))
-                scratch["n", c] = n[:].bitcast(I32)
-            elif kind == "frac":
-                r = work.tile([P, S], F32, name="frac")
-                nc.vector.scalar_tensor_tensor(
-                    out=r[:], in0=pos[:], scalar=col(turn, c), in1=scratch["n", c], op0=ALU.mult, op1=ALU.subtract
-                )
-                scratch["r", c] = r
-            elif kind == "cos":
-                a = work.tile([P, S], F32, name="absfrac")
-                nc.scalar.activation(out=a[:], in_=scratch["r", c][:], func=ACT.Abs)
-                sine(cos[c], a, -2.0 * math.pi, "halfpi")
+        def fold(in_, scale, bias_name):
+            a = work.tile([P, S], F32, name="folded")
+            if bias_name is None:
+                nc.scalar.activation(out=a[:], in_=in_[:], func=ACT.Abs, scale=scale)
             else:
-                sine(sin[c], scratch["r", c], -2.0 * math.pi)
+                nc.scalar.activation(out=a[:], in_=in_[:], func=ACT.Abs, scale=scale, bias=angle[bias_name][:])
+            return a
 
-        def table_plan(c):
-            hi = c + NPAIR
-            if hi >= FIRST_DIRECT:
-                upper = [("direct_cos", hi), ("direct_sin", hi)]
+        def upper_cos(c):
+            if c >= FIRST_DIRECT:
+                sine(cos[c], pos, col(nfrad, c), "halfpi")
             else:
-                upper = [("fold_cos", hi), ("fold_sin", hi)]
-            return [("turns", c)] + upper, [("frac", c)], [("cos", c), ("sin", c)]
+                sine(cos[c], fold(pos, col(frad, c), "negpi"), 1.0, "neghalfpi")
+
+        def upper_sin(c):
+            if c >= FIRST_DIRECT:
+                sine(sin[c], pos, col(frad, c))
+            else:
+                sine(sin[c], fold(pos, col(frad, c), "neghalfpi"), -1.0, "halfpi")
+
+        def lower_cos(c):
+            sine(cos[c], fold(frac[c], 1.0, None), -2.0 * math.pi, "halfpi")
+
+        def lower_sin(c):
+            sine(sin[c], frac[c], -2.0 * math.pi)
+
+        def whole_turns_vector(c):
+            n = work.tile([P, S], I32, name="turns_v", bufs=1)
+            nc.vector.tensor_scalar(out=n[:], in0=pos[:], scalar1=col(turn, c), scalar2=None, op0=ALU.mult)
+            turns[c] = n[:]
+
+        def whole_turns_scalar(c):
+            n = work.tile([P, S], U32, name="turns_s", bufs=5)
+            nc.scalar.activation(out=n[:], in_=pos[:], func=ACT.Copy, scale=col(turn, c))
+            turns[c] = n[:].bitcast(I32)
+
+        def fraction(c):
+            frac[c] = keep.tile([P, S], F32, name="frac%d" % c)
+            nc.vector.scalar_tensor_tensor(
+                out=frac[c][:], in0=pos[:], scalar=col(turn, c), in1=turns[c], op0=ALU.mult, op1=ALU.subtract
+            )
 
         units = [(m, c, b) for c in PAIR_ORDER for m in range(2) for b in range(NSEQ)]
         last = len(units) - 1
@@ -233,37 +240,64 @@ def tile_ropemultiheadattention_pa_kernel(
                     )
             return acc
 
-        def products(u, acc, h, t1, t2):
+        def products(u, acc, t1, t2, between=None):
             m, c, b = units[u]
-            blk = c + NPAIR * h
-            own = col(bias, NBLK * m + blk)
-            other = col(bias, NBLK * m + c + NPAIR * (1 - h))
-            nc.vector.scalar_tensor_tensor(
-                out=t1, in0=acc[h][:], scalar=own, in1=cos[blk][:], op0=ALU.add, op1=ALU.mult
-            )
-            nc.vector.scalar_tensor_tensor(
-                out=t2, in0=acc[1 - h][:], scalar=other, in1=sin[blk][:], op0=ALU.add, op1=ALU.mult
-            )
+            for src in (1, 0):
+                own = c + NPAIR * src
+                other = c + NPAIR * (1 - src)
+                steps = [(t1[src], cos[own]), (t2[1 - src], sin[other])]
+                if src == 0:
+                    steps = steps[::-1]
+                    if between is not None:
+                        between()
+                for dst, table in steps:
+                    nc.vector.scalar_tensor_tensor(
+                        out=dst, in0=acc[src][:], scalar=bias_col(m, own), in1=table[:], op0=ALU.add, op1=ALU.mult
+                    )
 
-        def rotate(u, acc):
-            if u == last or u in V_ADD_UNITS:
-                out = {}
-                for h in (1, 0):
-                    t1 = work.tile([P, S], F32, name="t1h", bufs=2)
-                    t2 = work.tile([P, S], F32, name="t2h", bufs=2)
-                    oh = work.tile([P, S], F32, name="oh", bufs=4)
-                    products(u, acc, h, t1[:], t2[:])
-                    engine = nc.gpsimd if h == 1 else nc.vector
-                    engine.tensor_tensor(out=oh[:], in0=t1[:], in1=t2[:], op=ALU.add)
-                    out[h] = oh[:]
-                return out
-            t1 = work.tile([P, 2, S], F32, name="t1", bufs=3)
-            t2 = work.tile([P, 2, S], F32, name="t2", bufs=3)
-            o = work.tile([P, 2, S], F32, name="o", bufs=6)
-            for h in (1, 0):
-                products(u, acc, h, t1[:, h, :], t2[:, h, :])
-            nc.gpsimd.tensor_tensor(out=o[:], in0=t1[:], in1=t2[:], op=ALU.add)
-            return {h: o[:, h, :] for h in (0, 1)}
+        rotated = {}
+
+        def halves(t, i):
+            return {h: t[:, 2 * i + h, :] for h in (0, 1)}
+
+        def rotate_pair(k, hooks):
+            us = (2 * k, 2 * k + 1)
+            wide = all(u not in NARROW_UNITS and u not in ACC_UNITS for u in us)
+            if wide:
+                t1 = work.tile([P, 4, S], F32, name="t1w", bufs=3)
+                t2 = work.tile([P, 4, S], F32, name="t2w", bufs=3)
+                ow = work.tile([P, 4, S], F32, name="ow", bufs=3)
+            for i, u in enumerate(us):
+                acc = project(u)
+                if not wide:
+                    t1 = work.tile([P, 2, S], F32, name="t1w", bufs=3)
+                    t2 = work.tile([P, 2, S], F32, name="t2w", bufs=3)
+                j = i if wide else 0
+                products(u, acc, halves(t1, j), halves(t2, j), hooks[1] if i == 1 else None)
+                if i == 0 and hooks[0] is not None:
+                    hooks[0]()
+                if wide:
+                    rotated[u] = {h: [ow[:, 2 * i + h, :]] for h in (0, 1)}
+                elif u in ACC_UNITS:
+                    rotated[u] = {h: [t1[:, h, :], t2[:, h, :]] for h in (0, 1)}
+                else:
+                    on = work.tile([P, 2, S], F32, name="ow", bufs=3)
+                    nc.gpsimd.tensor_tensor(out=on[:], in0=t1[:], in1=t2[:], op=ALU.add)
+                    rotated[u] = {h: [on[:, h, :]] for h in (0, 1)}
+            if wide:
+                nc.gpsimd.tensor_tensor(out=ow[:], in0=t1[:], in1=t2[:], op=ALU.add)
+
+        def turn_round(dst, u, h, t):
+            parts = rotated[u][h]
+            for i, part in enumerate(parts):
+                nc.tensor.matmul(
+                    out=dst,
+                    lhsT=part[:, P * t : P * (t + 1)],
+                    rhs=ident[:],
+                    is_transpose=True,
+                    start=(i == 0),
+                    stop=(i == len(parts) - 1),
+                )
 
         def store(u, h, t0, st):
             m, c, b = units[u]
@@ -277,11 +311,7 @@ def tile_ropemultiheadattention_pa_kernel(
                 for h in (1, 0):
                     tr[u, h] = psum_tr.tile([P, S], F32, name="tr")
                     for t in range(NT):
-                        nc.tensor.transpose(
-                            out=tr[u, h][:, P * t : P * (t + 1)],
-                            in_=rotated[u][h][:, P * t : P * (t + 1)],
-                            identity=ident[:],
-                        )
+                        turn_round(tr[u, h][:, P * t : P * (t + 1)], u, h, t)
             for u in batch:
                 for h in (1, 0):
                     st = work.tile([P, NT, P], F32, name="st", bufs=8)
@@ -294,11 +324,7 @@ def tile_ropemultiheadattention_pa_kernel(
                 for j in range(2):
                     tr[h, j] = psum_tr.tile([P, S], F32, name="tr")
                     for t in range(2):
-                        nc.tensor.transpose(
-                            out=tr[h, j][:, P * t : P * (t + 1)],
-                            in_=rotated[u][h][:, P * (2 * j + t) : P * (2 * j + t + 1)],
-                            identity=ident[:],
-                        )
+                        turn_round(tr[h, j][:, P * t : P * (t + 1)], u, h, 2 * j + t)
             for h in (1, 0):
                 for j in range(2):
                     st = work.tile([P, 2, P], F32, name="st2", bufs=4)
@@ -309,24 +335,38 @@ def tile_ropemultiheadattention_pa_kernel(
                         nc.scalar.copy(out=flat_st, in_=tr[h, j][:, 0 : 2 * P])
                     store(u, h, 2 * j, st)
 
-        for stretch in table_plan(FIRST):
-            for kind, c in stretch:
-                table_step(kind, c)
+        whole_turns_vector(PAIR_ORDER[0])
+        fraction(PAIR_ORDER[0])
+        upper_cos(FIRST + NPAIR)
+        upper_sin(FIRST + NPAIR)
+        whole_turns_scalar(PAIR_ORDER[1])
+        lower_sin(FIRST)
+        lower_cos(FIRST)
+        fraction(PAIR_ORDER[1])
+        for c in PAIR_ORDER[2:]:
+            whole_turns_scalar(c)
 
-        rotated = {}
-        for k in range(len(units) // 2):
-            plan = None
-            if k % 2 == 0 and k // 2 + 1 < NPAIR:
-                plan = table_plan(PAIR_ORDER[k // 2 + 1])
-                held = plan
-            rotated[2 * k] = rotate(2 * k, project(2 * k))
-            if k % 2 == 1 and k // 2 + 1 < NPAIR:
-                for kind, c in held[1] + held[2]:
-                    table_step(kind, c)
-            rotated[2 * k + 1] = rotate(2 * k + 1, project(2 * k + 1))
-            emit([u for u in (2 * k - 3, 2 * k - 2) if u >= 0])
-            if k % 2 == 0 and k // 2 + 1 < NPAIR:
-                for kind, c in held[0]:
-                    table_step(kind, c)
-        emit([last - 2, last - 1])
+        def fractions(cs):
+            def run():
+                for c in cs:
+                    fraction(c)
+            return run
+
+        npairs = len(units) // 2
+        for k in range(npairs):
+            more = k // 2 + 1 < NPAIR
+            nxt = PAIR_ORDER[k // 2 + 1] if more else None
+            hooks = (fractions(PAIR_ORDER[2:4]), fractions(PAIR_ORDER[4:6])) if k == 0 else (None, None)
+            if more and k % 2 == 1:
+                lower_sin(nxt)
+                lower_cos(nxt)
+            rotate_pair(k, hooks)
+            if k >= 2:
+                emit([2 * k - 4, 2 * k - 3])
+            if more and k % 2 == 0:
+                upper_cos(nxt + NPAIR)
+                upper_sin(nxt + NPAIR)
+        emit([last - 3])
+        emit([last - 1])
+        emit([last - 2])
         emit_last(last)

@@ -26,8 +26,8 @@ FREQ_BITS = 10
 FIRST_DIRECT = 7
 PAIR_ORDER = (5, 4, 3, 2, 1, 0)
 FIRST = PAIR_ORDER[0]
-NARROW_UNITS = (20, 21)
-ACC_UNITS = (22, 23)
+ACC_SLOTS = (1,) * 11 + (4,)
+WARM_MATMULS = 8
 FLOPS = 2 * NSEQ * S * D * 2 * E
 
 
@@ -93,6 +93,8 @@ def tile_ropemultiheadattention_pa_kernel(
 
         idx = keep.tile([P, NBLK], I32, name="idx")
         nc.gpsimd.iota(idx[:], pattern=[[-P, NBLK]], base=2 ** (FREQ_BITS + 1) - 1, channel_multiplier=-1)
+        zeros = keep.tile([P, S], BF16, name="zeros")
+        nc.gpsimd.memset(zeros[:], 0.0)
         ident = keep.tile([P, P], F32, name="ident")
         make_identity(nc, ident[:])
         pos = keep.tile([P, S], F32, name="pos")
@@ -111,6 +113,10 @@ def tile_ropemultiheadattention_pa_kernel(
         for m in range(2):
             for h in (1, 0):
                 load_codes(wc_rest[m][:, :, h, :], w_words[m], 2 * HALF * h)
+
+        idle_ps = psum_tr.tile([P, S], F32, name="tr")
+        for i in range(WARM_MATMULS):
+            nc.tensor.matmul(out=idle_ps[:], lhsT=zeros[:, 0:P], rhs=zeros[:], start=True, stop=True)
 
         brows32 = keep.tile([P, BIAS_ROW], F32, name="brows32")
         nc.scalar.copy(out=brows32[:], in_=brows[:])
@@ -204,7 +210,7 @@ def tile_ropemultiheadattention_pa_kernel(
             turns[c] = n[:]
 
         def whole_turns_scalar(c):
-            n = work.tile([P, S], U32, name="turns_s", bufs=5)
+            n = work.tile([P, S], U32, name="turns_s", bufs=2)
             nc.scalar.activation(out=n[:], in_=pos[:], func=ACT.Copy, scale=col(turn, c))
             turns[c] = n[:].bitcast(I32)
 
@@ -257,35 +263,32 @@ def tile_ropemultiheadattention_pa_kernel(
 
         rotated = {}
 
-        def halves(t, i):
-            return {h: t[:, 2 * i + h, :] for h in (0, 1)}
-
-        def rotate_pair(k, hooks):
-            us = (2 * k, 2 * k + 1)
-            wide = all(u not in NARROW_UNITS and u not in ACC_UNITS for u in us)
-            if wide:
-                t1 = work.tile([P, 4, S], F32, name="t1w", bufs=3)
-                t2 = work.tile([P, 4, S], F32, name="t2w", bufs=3)
-                ow = work.tile([P, 4, S], F32, name="ow", bufs=3)
-            for i, u in enumerate(us):
-                acc = project(u)
-                if not wide:
-                    t1 = work.tile([P, 2, S], F32, name="t1w", bufs=3)
-                    t2 = work.tile([P, 2, S], F32, name="t2w", bufs=3)
-                j = i if wide else 0
-                products(u, acc, halves(t1, j), halves(t2, j), hooks[1] if i == 1 else None)
-                if i == 0 and hooks[0] is not None:
-                    hooks[0]()
-                if wide:
-                    rotated[u] = {h: [ow[:, 2 * i + h, :]] for h in (0, 1)}
-                elif u in ACC_UNITS:
-                    rotated[u] = {h: [t1[:, h, :], t2[:, h, :]] for h in (0, 1)}
-                else:
-                    on = work.tile([P, 2, S], F32, name="ow", bufs=3)
-                    nc.gpsimd.tensor_tensor(out=on[:], in0=t1[:], in1=t2[:], op=ALU.add)
-                    rotated[u] = {h: [on[:, h, :]] for h in (0, 1)}
-            if wide:
-                nc.gpsimd.tensor_tensor(out=ow[:], in0=t1[:], in1=t2[:], op=ALU.add)
+        def rotate_pair(k, hook):
+            n_sum = 4 - ACC_SLOTS[k]
+            if n_sum > 0:
+                t1w = work.tile([P, n_sum, S], F32, name="t1w", bufs=3)
+                t2w = work.tile([P, n_sum, S], F32, name="t2w", bufs=3)
+                ow = work.tile([P, n_sum, S], F32, name="ow", bufs=3)
+            for i in range(2):
+                u = 2 * k + i
+                t1 = {}
+                t2 = {}
+                rotated[u] = {}
+                for h in (1, 0):
+                    slot = 2 * i + 1 - h
+                    if slot < n_sum:
+                        t1[h] = t1w[:, slot, :]
+                        t2[h] = t2w[:, slot, :]
+                        rotated[u][h] = [ow[:, slot, :]]
+                    else:
+                        t1a = work.tile([P, S], F32, name="t1a", bufs=6)
+                        t2a = work.tile([P, S], F32, name="t2a", bufs=6)
+                        t1[h] = t1a[:]
+                        t2[h] = t2a[:]
+                        rotated[u][h] = [t1a[:], t2a[:]]
+                products(u, project(u), t1, t2, hook if i == 1 else None)
+            if n_sum > 0:
+                nc.gpsimd.tensor_tensor(out=ow[:], in0=t1w[:], in1=t2w[:], op=ALU.add)
 
         def turn_round(dst, u, h, t):
             parts = rotated[u][h]
@@ -339,34 +342,30 @@ def tile_ropemultiheadattention_pa_kernel(
         fraction(PAIR_ORDER[0])
         upper_cos(FIRST + NPAIR)
         upper_sin(FIRST + NPAIR)
-        whole_turns_scalar(PAIR_ORDER[1])
         lower_sin(FIRST)
         lower_cos(FIRST)
-        fraction(PAIR_ORDER[1])
-        for c in PAIR_ORDER[2:]:
-            whole_turns_scalar(c)
+        whole_turns_scalar(PAIR_ORDER[1])
 
-        def fractions(cs):
+        def fraction_of(c):
             def run():
-                for c in cs:
-                    fraction(c)
+                fraction(c)
             return run
 
         npairs = len(units) // 2
         for k in range(npairs):
-            more = k // 2 + 1 < NPAIR
-            nxt = PAIR_ORDER[k // 2 + 1] if more else None
-            hooks = (fractions(PAIR_ORDER[2:4]), fractions(PAIR_ORDER[4:6])) if k == 0 else (None, None)
-            if more and k % 2 == 1:
+            j = k // 2 + 1
+            nxt = PAIR_ORDER[j] if j < NPAIR else None
+            if nxt is not None and k % 2 == 1:
                 lower_sin(nxt)
                 lower_cos(nxt)
-            rotate_pair(k, hooks)
+                if j + 1 < NPAIR:
+                    whole_turns_scalar(PAIR_ORDER[j + 1])
+            rotate_pair(k, fraction_of(nxt) if nxt is not None and k % 2 == 0 else None)
             if k >= 2:
                 emit([2 * k - 4, 2 * k - 3])
-            if more and k % 2 == 0:
+            if nxt is not None and k % 2 == 0:
                 upper_cos(nxt + NPAIR)
                 upper_sin(nxt + NPAIR)
-        emit([last - 3])
         emit([last - 1])
-        emit([last - 2])
+        emit([last - 3, last - 2])
         emit_last(last)

@@ -26,8 +26,9 @@ FREQ_BITS = 10
 FIRST_DIRECT = 7
 PAIR_ORDER = (5, 4, 3, 2, 1, 0)
 FIRST = PAIR_ORDER[0]
-ACC_SLOTS = (1,) * 11 + (4,)
+ACC_SLOTS = (0, 1) * 5 + (2, 4)
 WARM_MATMULS = 8
+HEAD_FRACTIONS = 4
 FLOPS = 2 * NSEQ * S * D * 2 * E
 
 
@@ -43,7 +44,7 @@ def tile_ropemultiheadattention_pa_kernel(
     with ExitStack() as ctx:
         keep = ctx.enter_context(tc.tile_pool(name="keep", bufs=1))
         work = ctx.enter_context(tc.tile_pool(name="work", bufs=2))
-        psum_acc = ctx.enter_context(tc.psum_pool(name="psum_acc", bufs=4))
+        psum_acc = ctx.enter_context(tc.psum_pool(name="psum_acc", bufs=2))
         psum_tr = ctx.enter_context(tc.psum_pool(name="psum_tr", bufs=4))
         ctx.enter_context(tc.manual_schedule())
 
@@ -205,7 +206,7 @@ def tile_ropemultiheadattention_pa_kernel(
             sine(sin[c], frac[c], -2.0 * math.pi)
 
         def whole_turns_vector(c):
-            n = work.tile([P, S], I32, name="turns_v", bufs=1)
+            n = work.tile([P, S], I32, name="turns_v", bufs=2)
             nc.vector.tensor_scalar(out=n[:], in0=pos[:], scalar1=col(turn, c), scalar2=None, op0=ALU.mult)
             turns[c] = n[:]
 
@@ -230,10 +231,11 @@ def tile_ropemultiheadattention_pa_kernel(
 
         def project(u):
             m, c, b = units[u]
-            acc = {}
+            bank_a = psum_acc.tile([P, S], F32, name="acc_a", bufs=2)
+            bank_b = psum_acc.tile([P, S], F32, name="acc_b", bufs=2)
+            acc = {1: bank_a, 0: bank_b} if (u // 2) % 2 == 0 else {1: bank_b, 0: bank_a}
             for h in (1, 0):
                 blk = c + NPAIR * h
-                acc[h] = psum_acc.tile([P, S], F32, name="acc")
                 for g in range(PASSES):
                     nc.tensor.matmul_mx(
                         out=acc[h][:],
@@ -248,15 +250,12 @@ def tile_ropemultiheadattention_pa_kernel(
 
         def products(u, acc, t1, t2, between=None):
             m, c, b = units[u]
-            for src in (1, 0):
+            for src in (0, 1):
                 own = c + NPAIR * src
                 other = c + NPAIR * (1 - src)
-                steps = [(t1[src], cos[own]), (t2[1 - src], sin[other])]
-                if src == 0:
-                    steps = steps[::-1]
-                    if between is not None:
-                        between()
-                for dst, table in steps:
+                if src == 1 and between is not None:
+                    between()
+                for dst, table in ((t1[src], cos[own]), (t2[1 - src], sin[other])):
                     nc.vector.scalar_tensor_tensor(
                         out=dst, in0=acc[src][:], scalar=bias_col(m, own), in1=table[:], op0=ALU.add, op1=ALU.mult
                     )
@@ -339,12 +338,14 @@ def tile_ropemultiheadattention_pa_kernel(
                     store(u, h, 2 * j, st)
 
         whole_turns_vector(PAIR_ORDER[0])
-        fraction(PAIR_ORDER[0])
+        for i in range(HEAD_FRACTIONS):
+            if i + 1 < HEAD_FRACTIONS:
+                whole_turns_vector(PAIR_ORDER[i + 1])
+            fraction(PAIR_ORDER[i])
         upper_cos(FIRST + NPAIR)
         upper_sin(FIRST + NPAIR)
         lower_sin(FIRST)
         lower_cos(FIRST)
-        whole_turns_scalar(PAIR_ORDER[1])
 
         def fraction_of(c):
             def run():
@@ -358,9 +359,9 @@ def tile_ropemultiheadattention_pa_kernel(
             if nxt is not None and k % 2 == 1:
                 lower_sin(nxt)
                 lower_cos(nxt)
-                if j + 1 < NPAIR:
+                if HEAD_FRACTIONS <= j + 1 < NPAIR:
                     whole_turns_scalar(PAIR_ORDER[j + 1])
-            rotate_pair(k, fraction_of(nxt) if nxt is not None and k % 2 == 0 else None)
+            rotate_pair(k, fraction_of(nxt) if nxt is not None and k % 2 == 0 and j >= HEAD_FRACTIONS else None)
             if k >= 2:
                 emit([2 * k - 4, 2 * k - 3])
             if nxt is not None and k % 2 == 0:

@@ -165,8 +165,14 @@ def tile_ropemultiheadattention_pa_kernel(
                 out=t[:], in0=p1[:], scalar=factor, in1=p5[:, 4, :], op0=ALU.mult, op1=ALU.mult
             )
 
-        cos = [keep.tile([P, S], F32, name="cos%d" % c) for c in range(NBLK)]
-        sin = [keep.tile([P, S], F32, name="sin%d" % c) for c in range(NBLK)]
+        tabs = [[keep.tile([P, 2, S], F32, name="tab%d_%d" % (c, s)) for s in range(2)] for c in range(NPAIR)]
+        cos = {}
+        sin = {}
+        for c in range(NPAIR):
+            cos[c] = tabs[c][0][:, 0, :]
+            sin[c + NPAIR] = tabs[c][0][:, 1, :]
+            sin[c] = tabs[c][1][:, 0, :]
+            cos[c + NPAIR] = tabs[c][1][:, 1, :]
         turns = {}
         frac = {}
 
@@ -175,9 +181,9 @@ def tile_ropemultiheadattention_pa_kernel(
 
         def sine(out, in_, scale, bias_name=None):
             if bias_name is None:
-                nc.scalar.activation(out=out[:], in_=in_[:], func=ACT.Sin, scale=scale)
+                nc.scalar.activation(out=out, in_=in_[:], func=ACT.Sin, scale=scale)
             else:
-                nc.scalar.activation(out=out[:], in_=in_[:], func=ACT.Sin, scale=scale, bias=angle[bias_name][:])
+                nc.scalar.activation(out=out, in_=in_[:], func=ACT.Sin, scale=scale, bias=angle[bias_name][:])
 
         def fold(in_, scale, bias_name):
             a = work.tile([P, S], F32, name="folded")
@@ -248,46 +254,39 @@ def tile_ropemultiheadattention_pa_kernel(
                     )
             return acc
 
-        def products(u, acc, t1, t2, between=None):
+        def products(u, acc, x, i, between=None):
             m, c, b = units[u]
             for src in (0, 1):
-                own = c + NPAIR * src
-                other = c + NPAIR * (1 - src)
                 if src == 1 and between is not None:
                     between()
-                for dst, table in ((t1[src], cos[own]), (t2[1 - src], sin[other])):
-                    nc.vector.scalar_tensor_tensor(
-                        out=dst, in0=acc[src][:], scalar=bias_col(m, own), in1=table[:], op0=ALU.add, op1=ALU.mult
-                    )
+                nc.vector.scalar_tensor_tensor(
+                    out=x[:, src, 2 * i : 2 * i + 2, :],
+                    in0=acc[src][:].unsqueeze(1).to_broadcast([P, 2, S]),
+                    scalar=bias_col(m, c + NPAIR * src),
+                    in1=tabs[c][src][:],
+                    op0=ALU.add,
+                    op1=ALU.mult,
+                )
 
         rotated = {}
 
         def rotate_pair(k, hook):
             n_sum = 4 - ACC_SLOTS[k]
+            x = work.tile([P, 2, 4, S], F32, name="x", bufs=3)
             if n_sum > 0:
-                t1w = work.tile([P, n_sum, S], F32, name="t1w", bufs=3)
-                t2w = work.tile([P, n_sum, S], F32, name="t2w", bufs=3)
                 ow = work.tile([P, n_sum, S], F32, name="ow", bufs=3)
             for i in range(2):
                 u = 2 * k + i
-                t1 = {}
-                t2 = {}
                 rotated[u] = {}
-                for h in (1, 0):
-                    slot = 2 * i + 1 - h
+                for h in (0, 1):
+                    slot = 2 * i + h
                     if slot < n_sum:
-                        t1[h] = t1w[:, slot, :]
-                        t2[h] = t2w[:, slot, :]
                         rotated[u][h] = [ow[:, slot, :]]
                     else:
-                        t1a = work.tile([P, S], F32, name="t1a", bufs=6)
-                        t2a = work.tile([P, S], F32, name="t2a", bufs=6)
-                        t1[h] = t1a[:]
-                        t2[h] = t2a[:]
-                        rotated[u][h] = [t1a[:], t2a[:]]
-                products(u, project(u), t1, t2, hook if i == 1 else None)
+                        rotated[u][h] = [x[:, 0, slot, :], x[:, 1, slot, :]]
+                products(u, project(u), x, i, hook if i == 1 else None)
             if n_sum > 0:
-                nc.gpsimd.tensor_tensor(out=ow[:], in0=t1w[:], in1=t2w[:], op=ALU.add)
+                nc.gpsimd.tensor_tensor(out=ow[:], in0=x[:, 0, 0:n_sum, :], in1=x[:, 1, 0:n_sum, :], op=ALU.add)
 
         def turn_round(dst, u, h, t):
             parts = rotated[u][h]

@@ -26,7 +26,7 @@ FREQ_BITS = 10
 FIRST_DIRECT = 7
 PAIR_ORDER = (5, 4, 3, 2, 1, 0)
 FIRST = PAIR_ORDER[0]
-ACC_SLOTS = (0, 1) * 5 + (2, 4)
+ACC_SLOTS = (0, 0, 0, 0, 0, 1, 0, 1, 0, 0, 2, 4)
 WARM_MATMULS = 8
 HEAD_FRACTIONS = 4
 FLOPS = 2 * NSEQ * S * D * 2 * E

@@ -284,7 +284,9 @@ def tile_ropemultiheadattention_pa_kernel(
                         rotated[u][h] = [ow[:, slot, :]]
                     else:
                         rotated[u][h] = [x[:, 0, slot, :], x[:, 1, slot, :]]
-                products(u, project(u), x, i, hook if i == 1 else None)
+                products(u, project(u), x, i)
+            if hook is not None:
+                hook()
             if n_sum > 0:
                 nc.gpsimd.tensor_tensor(out=ow[:], in0=x[:, 0, 0:n_sum, :], in1=x[:, 1, 0:n_sum, :], op=ALU.add)
 

@@ -85,8 +85,8 @@ def tile_ropemultiheadattention_pa_kernel(
         brows = keep.tile([P, BIAS_ROW], BF16, name="brows")
         nc.vector.memset(brows[:], 0.0)
         nc.vector.memset(warm[:], 0.0)
-        nc.vector.memset(flat(xs[0]).bitcast(I32), 0)
         nc.vector.memset(flat(ws[0]).bitcast(I32), 0)
+        nc.vector.memset(flat(xs[0]).bitcast(I32), 0)
 
         for m in range(2):
             nc.scalar.dma_start(out=brows[4 * m : 4 * m + 4, :], in_=biases[m].rearrange("(r n) -> r n", n=BIAS_ROW))
@@ -103,10 +103,10 @@ def tile_ropemultiheadattention_pa_kernel(
         nc.gpsimd.memset(flat(xs[1]).bitcast(F32), 0.0)
         nc.gpsimd.memset(flat(ws[1]).bitcast(F32), 0.0)
 
-        load_codes(xw[0][:, :, :], x_words, 0)
         load_first_codes(0)
-        load_planes(xs[0], x_scales, 0)
+        load_codes(xw[0][:, :, :], x_words, 0)
         load_planes(ws[0], w_scales[0], 0)
+        load_planes(xs[0], x_scales, 0)
         load_planes(xs[1], x_scales, S)
         load_codes(xw[1][:, :, :], x_words, 2 * S)
         load_planes(ws[1], w_scales[1], 0)

@@ -26,9 +26,10 @@ FREQ_BITS = 10
 FIRST_DIRECT = 7
 PAIR_ORDER = (5, 4, 3, 2, 1, 0)
 FIRST = PAIR_ORDER[0]
-ACC_SLOTS = (0, 0, 0, 0, 0, 1, 0, 1, 0, 0, 2, 4)
+ACC_SLOTS = (0, 0, 0, 1, 0, 1, 0, 1, 0, 0, 2, 4)
 WARM_MATMULS = 8
-HEAD_FRACTIONS = 4
+HEAD_FRACTIONS = 3
+EARLY_STEPS = 2
 FLOPS = 2 * NSEQ * S * D * 2 * E
 
 
@@ -44,8 +45,7 @@ def tile_ropemultiheadattention_pa_kernel(
     with ExitStack() as ctx:
         keep = ctx.enter_context(tc.tile_pool(name="keep", bufs=1))
         work = ctx.enter_context(tc.tile_pool(name="work", bufs=2))
-        psum_acc = ctx.enter_context(tc.psum_pool(name="psum_acc", bufs=2))
-        psum_tr = ctx.enter_context(tc.psum_pool(name="psum_tr", bufs=4))
+        psum = ctx.enter_context(tc.psum_pool(name="psum", bufs=8))
         ctx.enter_context(tc.manual_schedule())
 
         xw = [keep.tile([P, PASSES, 2 * S], U8, name="xw%d" % b, align_bytes=64) for b in range(NSEQ)]
@@ -115,13 +115,13 @@ def tile_ropemultiheadattention_pa_kernel(
             for h in (1, 0):
                 load_codes(wc_rest[m][:, :, h, :], w_words[m], 2 * HALF * h)
 
-        idle_ps = psum_tr.tile([P, S], F32, name="tr")
+        idle_ps = psum.tile([P, S], F32, name="bank")
         for i in range(WARM_MATMULS):
             nc.tensor.matmul(out=idle_ps[:], lhsT=zeros[:, 0:P], rhs=zeros[:], start=True, stop=True)
 
         brows32 = keep.tile([P, BIAS_ROW], F32, name="brows32")
         nc.scalar.copy(out=brows32[:], in_=brows[:])
-        bias_ps = psum_tr.tile([P, S], F32, name="tr")
+        bias_ps = psum.tile([P, S], F32, name="bank")
         for j in range(3):
             nc.tensor.transpose(
                 out=bias_ps[:, P * j : P * (j + 1)], in_=brows32[:, P * j : P * (j + 1)], identity=ident[:]
@@ -237,9 +237,10 @@ def tile_ropemultiheadattention_pa_kernel(
 
         def project(u):
             m, c, b = units[u]
-            bank_a = psum_acc.tile([P, S], F32, name="acc_a", bufs=2)
-            bank_b = psum_acc.tile([P, S], F32, name="acc_b", bufs=2)
-            acc = {1: bank_a, 0: bank_b} if (u // 2) % 2 == 0 else {1: bank_b, 0: bank_a}
+            bank_a = psum.tile([P, S], F32, name="bank")
+            bank_b = psum.tile([P, S], F32, name="bank")
+            swap = (u // 2) % 2 == 1 if u % 2 == 1 or u == 0 else (u // 2) % 2 == 0
+            acc = {1: bank_b, 0: bank_a} if swap else {1: bank_a, 0: bank_b}
             for h in (1, 0):
                 blk = c + NPAIR * h
                 for g in range(PASSES):
@@ -254,11 +255,9 @@ def tile_ropemultiheadattention_pa_kernel(
                     )
             return acc
 
-        def products(u, acc, x, i, between=None):
+        def products(u, acc, x, i):
             m, c, b = units[u]
-            for src in (0, 1):
-                if src == 1 and between is not None:
-                    between()
+            for src in (1, 0) if u == 0 else (0, 1):
                 nc.vector.scalar_tensor_tensor(
                     out=x[:, src, 2 * i : 2 * i + 2, :],
                     in0=acc[src][:].unsqueeze(1).to_broadcast([P, 2, S]),
@@ -285,9 +284,16 @@ def tile_ropemultiheadattention_pa_kernel(
                     else:
                         rotated[u][h] = [x[:, 0, slot, :], x[:, 1, slot, :]]
                 products(u, project(u), x, i)
+                if k < EARLY_STEPS:
+                    nc.gpsimd.tensor_tensor(
+                        out=ow[:, 2 * i : 2 * i + 2, :],
+                        in0=x[:, 0, 2 * i : 2 * i + 2, :],
+                        in1=x[:, 1, 2 * i : 2 * i + 2, :],
+                        op=ALU.add,
+                    )
             if hook is not None:
                 hook()
-            if n_sum > 0:
+            if n_sum > 0 and k >= EARLY_STEPS:
                 nc.gpsimd.tensor_tensor(out=ow[:], in0=x[:, 0, 0:n_sum, :], in1=x[:, 1, 0:n_sum, :], op=ALU.add)
 
         def turn_round(dst, u, h, t):
@@ -312,7 +318,7 @@ def tile_ropemultiheadattention_pa_kernel(
             tr = {}
             for u in batch:
                 for h in (1, 0):
-                    tr[u, h] = psum_tr.tile([P, S], F32, name="tr")
+                    tr[u, h] = psum.tile([P, S], F32, name="bank")
                     for t in range(NT):
                         turn_round(tr[u, h][:, P * t : P * (t + 1)], u, h, t)
             for u in batch:
@@ -325,14 +331,14 @@ def tile_ropemultiheadattention_pa_kernel(
             tr = {}
             for h in (1, 0):
                 for j in range(2):
-                    tr[h, j] = psum_tr.tile([P, S], F32, name="tr")
+                    tr[h, j] = psum.tile([P, S], F32, name="bank")
                     for t in range(2):
                         turn_round(tr[h, j][:, P * t : P * (t + 1)], u, h, 2 * j + t)
             for h in (1, 0):
                 for j in range(2):
                     st = work.tile([P, 2, P], F32, name="st2", bufs=4)
                     flat_st = st[:].rearrange("p t e -> p (t e)")
-                    if h == 0 and j == 1:
+                    if j == 1:
                         nc.vector.tensor_copy(out=flat_st, in_=tr[h, j][:, 0 : 2 * P])
                     else:
                         nc.scalar.copy(out=flat_st, in_=tr[h, j][:, 0 : 2 * P])

@@ -26,7 +26,11 @@ FREQ_BITS = 10
 FIRST_DIRECT = 7
 PAIR_ORDER = (5, 4, 3, 2, 1, 0)
 FIRST = PAIR_ORDER[0]
-ACC_SLOTS = (0, 0, 0, 1, 0, 1, 0, 1, 0, 0, 2, 4)
+GROUPS = ((5,), (4,), (3,), (2,), (1, 0))
+TABLES_BEFORE = {1: (("lower", 4),), 3: (("lower", 3), ("turns", 2), ("turns", 1)), 5: (("lower", 2), ("turns", 0)), 6: (("lower", 1),), 7: (("lower", 0),)}
+TABLES_AFTER = {0: (("upper", 4), ("upper", 3)), 1: (("upper", 2), ("upper", 1)), 2: (("upper", 0),)}
+FRACTION_BEHIND = {4: 2, 5: 1, 6: 0}
+ACC_SLOTS = (0, 0, 0, 1, 1, 1, 0, 0, 0, 0, 2, 4)
 WARM_MATMULS = 8
 HEAD_FRACTIONS = 3
 EARLY_STEPS = 2
@@ -227,7 +231,8 @@ def tile_ropemultiheadattention_pa_kernel(
                 out=frac[c][:], in0=pos[:], scalar=col(turn, c), in1=turns[c], op0=ALU.mult, op1=ALU.subtract
             )
 
-        units = [(m, c, b) for c in PAIR_ORDER for m in range(2) for b in range(NSEQ)]
+        units = [(m, c, b) for group in GROUPS for m in range(2) for b in range(NSEQ) for c in group]
+        joined = [len(group) == 2 for group in GROUPS for i in range(2 * len(group))]
         last = len(units) - 1
 
         def w_codes(m, c, h, g):
@@ -327,6 +332,23 @@ def tile_ropemultiheadattention_pa_kernel(
                     nc.scalar.copy(out=st[:].rearrange("p t e -> p (t e)"), in_=tr[u, h][:])
                     store(u, h, 0, st)
 
+        def emit_joined(k):
+            m, c, b = units[2 * k + 1]
+            rows = outs[m][b].rearrange("(t p) e -> p t e", p=P)
+            tr = {}
+            for h in (1, 0):
+                for j in range(2):
+                    tr[h, j] = psum.tile([P, S], F32, name="bank")
+                    for t in range(2):
+                        for i in range(2):
+                            turn_round(tr[h, j][:, P * (2 * t + i) : P * (2 * t + i + 1)], 2 * k + 1 - i, h, 2 * j + t)
+            for h in (1, 0):
+                blk = c + NPAIR * h
+                for j in range(2):
+                    st = work.tile([P, 2, 2 * P], F32, name="st", bufs=8)
+                    nc.scalar.copy(out=st[:].rearrange("p t e -> p (t e)"), in_=tr[h, j][:])
+                    nc.sync.dma_start(out=rows[:, 2 * j : 2 * j + 2, P * blk : P * (blk + 2)], in_=st[:])
+
         def emit_last(u):
             tr = {}
             for h in (1, 0):
@@ -359,21 +381,30 @@ def tile_ropemultiheadattention_pa_kernel(
                 fraction(c)
             return run
 
+        def make_tables(jobs):
+            for kind, c in jobs:
+                if kind == "upper":
+                    upper_cos(c + NPAIR)
+                    upper_sin(c + NPAIR)
+                elif kind == "lower":
+                    lower_sin(c)
+                    lower_cos(c)
+                else:
+                    whole_turns_scalar(c)
+
+        def emit_step(k):
+            if joined[k]:
+                emit_joined(k)
+            else:
+                emit([2 * k, 2 * k + 1])
+
         npairs = len(units) // 2
         for k in range(npairs):
-            j = k // 2 + 1
-            nxt = PAIR_ORDER[j] if j < NPAIR else None
-            if nxt is not None and k % 2 == 1:
-                lower_sin(nxt)
-                lower_cos(nxt)
-                if HEAD_FRACTIONS <= j + 1 < NPAIR:
-                    whole_turns_scalar(PAIR_ORDER[j + 1])
-            rotate_pair(k, fraction_of(nxt) if nxt is not None and k % 2 == 0 and j >= HEAD_FRACTIONS else None)
+            make_tables(TABLES_BEFORE.get(k, ()))
+            rotate_pair(k, fraction_of(FRACTION_BEHIND[k]) if k in FRACTION_BEHIND else None)
             if k >= 2:
-                emit([2 * k - 4, 2 * k - 3])
-            if nxt is not None and k % 2 == 0:
-                upper_cos(nxt + NPAIR)
-                upper_sin(nxt + NPAIR)
+                emit_step(k - 2)
+            make_tables(TABLES_AFTER.get(k, ()))
         emit([last - 1])
-        emit([last - 3, last - 2])
+        emit_step(npairs - 2)
         emit_last(last)

@@ -30,7 +30,7 @@ GROUPS = ((5,), (4,), (3,), (2,), (1, 0))
 TABLES_BEFORE = {1: (("lower", 4),), 3: (("lower", 3), ("turns", 2), ("turns", 1)), 5: (("lower", 2), ("turns", 0)), 6: (("lower", 1),), 7: (("lower", 0),)}
 TABLES_AFTER = {0: (("upper", 4), ("upper", 3)), 1: (("upper", 2), ("upper", 1)), 2: (("upper", 0),)}
 FRACTION_BEHIND = {4: 2, 5: 1, 6: 0}
-ACC_SLOTS = (0, 0, 0, 1, 1, 1, 0, 0, 0, 0, 2, 4)
+ACC_SLOTS = (0, 0, 0, 0, 0, 0, 0, 0, 0, 0, 2, 4)
 WARM_MATMULS = 8
 HEAD_FRACTIONS = 3
 EARLY_STEPS = 2

@@ -274,7 +274,7 @@ def tile_ropemultiheadattention_pa_kernel(
 
         rotated = {}
 
-        def rotate_pair(k, hook):
+        def rotate_pair(k, hook, between):
             n_sum = 4 - ACC_SLOTS[k]
             x = work.tile([P, 2, 4, S], F32, name="x", bufs=3)
             if n_sum > 0:
@@ -289,6 +289,8 @@ def tile_ropemultiheadattention_pa_kernel(
                     else:
                         rotated[u][h] = [x[:, 0, slot, :], x[:, 1, slot, :]]
                 products(u, project(u), x, i)
+                if i == 0 and between is not None:
+                    between()
                 if k < EARLY_STEPS:
                     nc.gpsimd.tensor_tensor(
                         out=ow[:, 2 * i : 2 * i + 2, :],
@@ -398,13 +400,21 @@ def tile_ropemultiheadattention_pa_kernel(
             else:
                 emit([2 * k, 2 * k + 1])
 
+        def emit_step_of(k):
+            def run():
+                emit_step(k)
+            return run
+
         npairs = len(units) // 2
         for k in range(npairs):
             make_tables(TABLES_BEFORE.get(k, ()))
-            rotate_pair(k, fraction_of(FRACTION_BEHIND[k]) if k in FRACTION_BEHIND else None)
-            if k >= 2:
+            at_end = k == npairs - 1
+            rotate_pair(
+                k, fraction_of(FRACTION_BEHIND[k]) if k in FRACTION_BEHIND else None, emit_step_of(k - 2) if at_end else None
+            )
+            if k >= 2 and not at_end:
                 emit_step(k - 2)
             make_tables(TABLES_AFTER.get(k, ()))
-        emit([last - 1])
         emit_step(npairs - 2)
+        emit([last - 1])
         emit_last(last)

@@ -32,6 +32,7 @@ TABLES_AFTER = {0: (("upper", 4), ("upper", 3)), 1: (("upper", 2), ("upper", 1))
 FRACTION_BEHIND = {4: 2, 5: 1, 6: 0}
 ACC_SLOTS = (0, 0, 0, 0, 0, 0, 0, 0, 0, 0, 2, 4)
 WARM_MATMULS = 8
+BRIDGE_MATMULS = 4
 HEAD_FRACTIONS = 3
 EARLY_STEPS = 2
 FLOPS = 2 * NSEQ * S * D * 2 * E
@@ -130,6 +131,8 @@ def tile_ropemultiheadattention_pa_kernel(
             nc.tensor.transpose(
                 out=bias_ps[:, P * j : P * (j + 1)], in_=brows32[:, P * j : P * (j + 1)], identity=ident[:]
             )
+        for i in range(BRIDGE_MATMULS):
+            nc.tensor.matmul(out=idle_ps[:], lhsT=zeros[:, 0:P], rhs=zeros[:], start=True, stop=True)
         bias = keep.tile([P, 3, 8], F32, name="bias")
         nc.scalar.copy(out=bias[:], in_=bias_ps[:, 0:BIAS_ROW].rearrange("p (j r) -> p j r", j=3)[:, :, 0:8])
 

@@ -247,8 +247,7 @@ def tile_ropemultiheadattention_pa_kernel(
             m, c, b = units[u]
             bank_a = psum.tile([P, S], F32, name="bank")
             bank_b = psum.tile([P, S], F32, name="bank")
-            swap = (u // 2) % 2 == 1 if u % 2 == 1 or u == 0 else (u // 2) % 2 == 0
-            acc = {1: bank_b, 0: bank_a} if swap else {1: bank_a, 0: bank_b}
+            acc = {1: bank_a, 0: bank_b}
             for h in (1, 0):
                 blk = c + NPAIR * h
                 for g in range(PASSES):
@@ -265,7 +264,7 @@ def tile_ropemultiheadattention_pa_kernel(
 
         def products(u, acc, x, i):
             m, c, b = units[u]
-            for src in (1, 0) if u == 0 else (0, 1):
+            for src in (1, 0):
                 nc.vector.scalar_tensor_tensor(
                     out=x[:, src, 2 * i : 2 * i + 2, :],
                     in0=acc[src][:].unsqueeze(1).to_broadcast([P, 2, S]),

@@ -50,11 +50,12 @@ def tile_ropemultiheadattention_pa_kernel(
     with ExitStack() as ctx:
         keep = ctx.enter_context(tc.tile_pool(name="keep", bufs=1))
         work = ctx.enter_context(tc.tile_pool(name="work", bufs=2))
+        far = ctx.enter_context(tc.tile_pool(name="far", bufs=1))
         psum = ctx.enter_context(tc.psum_pool(name="psum", bufs=8))
         ctx.enter_context(tc.manual_schedule())
 
-        xw = [keep.tile([P, PASSES, 2 * S], U8, name="xw%d" % b, align_bytes=64) for b in range(NSEQ)]
-        xs = [keep.tile([P, PASSES, S], U8, name="xs%d" % b, align_bytes=64) for b in range(NSEQ)]
+        xw = [far.tile([P, PASSES, 2 * S], U8, name="xw%d" % b, align_bytes=64) for b in range(NSEQ)]
+        xs = [far.tile([P, PASSES, S], U8, name="xs%d" % b, align_bytes=64) for b in range(NSEQ)]
         ws = [keep.tile([P, PASSES, E], U8, name="ws%d" % m, align_bytes=64) for m in range(2)]
         wc_first = [keep.tile([P, PASSES, 2, 2 * P], U8, name="wcf%d" % m, align_bytes=64) for m in range(2)]
         wc_rest = [

@@ -33,6 +33,7 @@ FRACTION_BEHIND = {4: 2, 5: 1, 6: 0}
 ACC_SLOTS = (0, 0, 0, 0, 0, 0, 0, 0, 0, 0, 2, 4)
 WARM_MATMULS = 8
 BRIDGE_MATMULS = 4
+SPACER_COLUMNS = 128
 HEAD_FRACTIONS = 3
 EARLY_STEPS = 2
 FLOPS = 2 * NSEQ * S * D * 2 * E
@@ -244,10 +245,20 @@ def tile_ropemultiheadattention_pa_kernel(
                 return wc_first[m][:, g, h, :]
             return wc_rest[m][:, g, h, 2 * P * c : 2 * P * (c + 1)]
 
+        last_kind = ["mx"]
+
+        def spacer(bank, kind):
+            if last_kind[0] != kind:
+                nc.tensor.matmul(
+                    out=bank[:, 0:SPACER_COLUMNS], lhsT=zeros[:, 0:P], rhs=zeros[:, 0:SPACER_COLUMNS], start=True, stop=True
+                )
+            last_kind[0] = kind
+
         def project(u):
             m, c, b = units[u]
             bank_a = psum.tile([P, S], F32, name="bank")
             bank_b = psum.tile([P, S], F32, name="bank")
+            spacer(bank_a, "mx")
             acc = {1: bank_a, 0: bank_b}
             for h in (1, 0):
                 blk = c + NPAIR * h
@@ -329,6 +340,7 @@ def tile_ropemultiheadattention_pa_kernel(
             for u in batch:
                 for h in (1, 0):
                     tr[u, h] = psum.tile([P, S], F32, name="bank")
+                    spacer(tr[u, h], "transpose")
                     for t in range(NT):
                         turn_round(tr[u, h][:, P * t : P * (t + 1)], u, h, t)
             for u in batch:
@@ -344,6 +356,7 @@ def tile_ropemultiheadattention_pa_kernel(
             for h in (1, 0):
                 for j in range(2):
                     tr[h, j] = psum.tile([P, S], F32, name="bank")
+                    spacer(tr[h, j], "transpose")
                     for t in range(2):
                         for i in range(2):
                             turn_round(tr[h, j][:, P * (2 * t + i) : P * (2 * t + i + 1)], 2 * k + 1 - i, h, 2 * j + t)
@@ -359,6 +372,7 @@ def tile_ropemultiheadattention_pa_kernel(
             for h in (1, 0):
                 for j in range(2):
                     tr[h, j] = psum.tile([P, S], F32, name="bank")
+                    spacer(tr[h, j], "transpose")
                     for t in range(2):
                         turn_round(tr[h, j][:, P * t : P * (t + 1)], u, h, 2 * j + t)
             for h in (1, 0):

@@ -33,7 +33,7 @@ FRACTION_BEHIND = {4: 2, 5: 1, 6: 0}
 ACC_SLOTS = (0, 0, 0, 0, 0, 0, 0, 0, 0, 0, 2, 4)
 WARM_MATMULS = 8
 BRIDGE_MATMULS = 4
-SPACER_COLUMNS = 128
+SPACER_COLUMNS = 64
 HEAD_FRACTIONS = 3
 EARLY_STEPS = 2
 FLOPS = 2 * NSEQ * S * D * 2 * E

@@ -22,7 +22,7 @@ NBLK = E // P
 NPAIR = NBLK // 2
 NT = S // P
 BIAS_ROW = 3 * P
-FREQ_BITS = 10
+FREQ_BITS = 6
 FIRST_DIRECT = 7
 PAIR_ORDER = (5, 4, 3, 2, 1, 0)
 FIRST = PAIR_ORDER[0]
@@ -58,7 +58,10 @@ def tile_ropemultiheadattention_pa_kernel(
         xw = [far.tile([P, PASSES, 2 * S], U8, name="xw%d" % b, align_bytes=64) for b in range(NSEQ)]
         xs = [far.tile([P, PASSES, S], U8, name="xs%d" % b, align_bytes=64) for b in range(NSEQ)]
         ws = [keep.tile([P, PASSES, E], U8, name="ws%d" % m, align_bytes=64) for m in range(2)]
-        wc_first = [keep.tile([P, PASSES, 2, 2 * P], U8, name="wcf%d" % m, align_bytes=64) for m in range(2)]
+        wc_first = [
+            [keep.tile([P, PASSES, 2 * P], U8, name="wcf%d_%d" % (m, h), align_bytes=64) for h in range(2)]
+            for m in range(2)
+        ]
         wc_rest = [
             keep.tile([P, PASSES, 2, 2 * P * FIRST], U8, name="wcr%d" % m, align_bytes=64) for m in range(2)
         ]
@@ -83,41 +86,42 @@ def tile_ropemultiheadattention_pa_kernel(
                     .bitcast(I32),
                 )
 
-        def load_first_codes(m):
-            for h in (1, 0):
-                load_codes(wc_first[m][:, :, h, :], w_words[m], 2 * P * (FIRST + NPAIR * h))
+        def load_first_codes(m, h):
+            load_codes(wc_first[m][h][:, :, :], w_words[m], 2 * P * (FIRST + NPAIR * h))
 
         warm = keep.tile([P, 1], F32, name="warm")
         warm_out = keep.tile([P, 1], F32, name="warm_out")
         brows = keep.tile([P, BIAS_ROW], BF16, name="brows")
         nc.vector.memset(brows[:], 0.0)
         nc.vector.memset(warm[:], 0.0)
-        nc.vector.memset(flat(ws[0]).bitcast(I32), 0)
         nc.vector.memset(flat(xs[0]).bitcast(I32), 0)
+        nc.vector.memset(flat(ws[0]).bitcast(I32), 0)
 
+        load_first_codes(0, 1)
         for m in range(2):
             nc.scalar.dma_start(out=brows[4 * m : 4 * m + 4, :], in_=biases[m].rearrange("(r n) -> r n", n=BIAS_ROW))
         nc.scalar.activation(out=warm_out[:], in_=warm[:], func=ACT.Sin)
 
-        idx = keep.tile([P, NBLK], I32, name="idx")
-        nc.gpsimd.iota(idx[:], pattern=[[-P, NBLK]], base=2 ** (FREQ_BITS + 1) - 1, channel_multiplier=-1)
+        idx = keep.tile([P, 1], I32, name="idx")
+        nc.gpsimd.iota(idx[:], pattern=[[1, 1]], base=P - 1, channel_multiplier=-1)
         zeros = keep.tile([P, S], BF16, name="zeros")
         nc.gpsimd.memset(zeros[:], 0.0)
-        ident = keep.tile([P, P], F32, name="ident")
-        make_identity(nc, ident[:])
         pos = keep.tile([P, S], F32, name="pos")
         nc.gpsimd.iota(pos[:], pattern=[[1, S]], base=0, channel_multiplier=0, allow_small_or_imprecise_dtypes=True)
+        ident = keep.tile([P, P], F32, name="ident")
+        make_identity(nc, ident[:])
         nc.gpsimd.memset(flat(xs[1]).bitcast(F32), 0.0)
         nc.gpsimd.memset(flat(ws[1]).bitcast(F32), 0.0)
 
-        load_first_codes(0)
+        load_planes(xs[0], x_scales, 0)
         load_codes(xw[0][:, :, :], x_words, 0)
         load_planes(ws[0], w_scales[0], 0)
-        load_planes(xs[0], x_scales, 0)
+        load_first_codes(0, 0)
         load_planes(xs[1], x_scales, S)
         load_codes(xw[1][:, :, :], x_words, 2 * S)
         load_planes(ws[1], w_scales[1], 0)
-        load_first_codes(1)
+        load_first_codes(1, 1)
+        load_first_codes(1, 0)
         for m in range(2):
             for h in (1, 0):
                 load_codes(wc_rest[m][:, :, h, :], w_words[m], 2 * HALF * h)
@@ -141,38 +145,35 @@ def tile_ropemultiheadattention_pa_kernel(
         def bias_col(m, blk):
             return bias[:, blk % 3, 4 * m + blk // 3 : 4 * m + blk // 3 + 1]
 
-        one = keep.tile([P, 1], F32, name="one")
-        nc.vector.memset(one[:], 1.0)
-        bit = keep.tile([P, FREQ_BITS, NBLK], I32, name="bit")
-        fac = keep.tile([P, FREQ_BITS, NBLK], F32, name="fac")
+        bit = keep.tile([P, FREQ_BITS], I32, name="bit")
+        fac = keep.tile([P, FREQ_BITS], F32, name="fac")
         for k in range(FREQ_BITS):
             nc.vector.tensor_scalar(
-                out=bit[:, k, :], in0=idx[:], scalar1=k + 1, scalar2=1,
+                out=bit[:, k : k + 1], in0=idx[:], scalar1=k + 1, scalar2=1,
                 op0=ALU.logical_shift_right, op1=ALU.bitwise_and,
             )
         for k in range(FREQ_BITS):
             nc.vector.tensor_scalar(
-                out=fac[:, k, :], in0=bit[:, k, :], scalar1=ROPE_BASE ** ((2.0 ** k) / HALF) - 1.0, scalar2=1.0,
+                out=fac[:, k : k + 1], in0=bit[:, k : k + 1], scalar1=ROPE_BASE ** ((2.0 ** k) / HALF) - 1.0, scalar2=1.0,
                 op0=ALU.mult, op1=ALU.add,
             )
-        angle = {}
-        for name, value in (("halfpi", math.pi / 2), ("neghalfpi", -math.pi / 2), ("negpi", -math.pi)):
-            angle[name] = keep.tile([P, 1], F32, name=name)
-            nc.vector.tensor_scalar(out=angle[name][:], in0=one[:], scalar1=value, scalar2=None, op0=ALU.mult)
-        p5 = keep.tile([P, 5, NBLK], F32, name="p5")
-        p2 = keep.tile([P, 2, NBLK], F32, name="p2")
-        p1 = keep.tile([P, NBLK], F32, name="p1")
-        nc.vector.tensor_tensor(out=p5[:], in0=fac[:, 0:5, :], in1=fac[:, 5:10, :], op=ALU.mult)
-        nc.vector.tensor_tensor(out=p2[:], in0=p5[:, 0:2, :], in1=p5[:, 2:4, :], op=ALU.mult)
-        nc.vector.tensor_tensor(out=p1[:], in0=p2[:, 0, :], in1=p2[:, 1, :], op=ALU.mult)
+        p3 = keep.tile([P, 3], F32, name="p3")
+        p1 = keep.tile([P, 1], F32, name="p1")
+        gfac = keep.tile([P, 1], F32, name="gfac")
+        nc.vector.tensor_tensor(out=p3[:], in0=fac[:, 0:3], in1=fac[:, 3:6], op=ALU.mult)
+        nc.vector.tensor_tensor(out=p1[:], in0=p3[:, 0:1], in1=p3[:, 1:2], op=ALU.mult)
         lowest = ROPE_BASE ** (-(2.0 ** FREQ_BITS - 1.0) / HALF)
-        turn = keep.tile([P, NBLK], F32, name="turn")
-        frad = keep.tile([P, NBLK], F32, name="frad")
-        nfrad = keep.tile([P, NBLK], F32, name="nfrad")
-        for t, factor in ((turn, lowest * 0.5 / math.pi), (frad, lowest), (nfrad, -lowest)):
-            nc.vector.scalar_tensor_tensor(
-                out=t[:], in0=p1[:], scalar=factor, in1=p5[:, 4, :], op0=ALU.mult, op1=ALU.mult
-            )
+        nc.vector.scalar_tensor_tensor(
+            out=gfac[:], in0=p1[:], scalar=lowest, in1=p3[:, 2:3], op0=ALU.mult, op1=ALU.mult
+        )
+        posg = keep.tile([P, S], F32, name="posg")
+        nc.vector.tensor_scalar(out=posg[:], in0=pos[:], scalar1=gfac[:, 0:1], scalar2=None, op0=ALU.mult)
+
+        def frad(c):
+            return ROPE_BASE ** (-c / float(NBLK))
+
+        def turn(c):
+            return frad(c) * 0.5 / math.pi
 
         tabs = [[keep.tile([P, 2, S], F32, name="tab%d_%d" % (c, s)) for s in range(2)] for c in range(NPAIR)]
         cos = {}
@@ -185,55 +186,46 @@ def tile_ropemultiheadattention_pa_kernel(
         turns = {}
         frac = {}
 
-        def col(t, c):
-            return t[:, c : c + 1]
+        def sine(out, in_, scale, bias=0.0):
+            nc.scalar.activation(out=out, in_=in_[:], func=ACT.Sin, scale=scale, bias=bias)
 
-        def sine(out, in_, scale, bias_name=None):
-            if bias_name is None:
-                nc.scalar.activation(out=out, in_=in_[:], func=ACT.Sin, scale=scale)
-            else:
-                nc.scalar.activation(out=out, in_=in_[:], func=ACT.Sin, scale=scale, bias=angle[bias_name][:])
-
-        def fold(in_, scale, bias_name):
+        def fold(in_, scale, bias=0.0):
             a = work.tile([P, S], F32, name="folded")
-            if bias_name is None:
-                nc.scalar.activation(out=a[:], in_=in_[:], func=ACT.Abs, scale=scale)
-            else:
-                nc.scalar.activation(out=a[:], in_=in_[:], func=ACT.Abs, scale=scale, bias=angle[bias_name][:])
+            nc.scalar.activation(out=a[:], in_=in_[:], func=ACT.Abs, scale=scale, bias=bias)
             return a
 
         def upper_cos(c):
             if c >= FIRST_DIRECT:
-                sine(cos[c], pos, col(nfrad, c), "halfpi")
+                sine(cos[c], posg, -frad(c), math.pi / 2)
             else:
-                sine(cos[c], fold(pos, col(frad, c), "negpi"), 1.0, "neghalfpi")
+                sine(cos[c], fold(posg, frad(c), -math.pi), 1.0, -math.pi / 2)
 
         def upper_sin(c):
             if c >= FIRST_DIRECT:
-                sine(sin[c], pos, col(frad, c))
+                sine(sin[c], posg, frad(c))
             else:
-                sine(sin[c], fold(pos, col(frad, c), "neghalfpi"), -1.0, "halfpi")
+                sine(sin[c], fold(posg, frad(c), -math.pi / 2), -1.0, math.pi / 2)
 
         def lower_cos(c):
-            sine(cos[c], fold(frac[c], 1.0, None), -2.0 * math.pi, "halfpi")
+            sine(cos[c], fold(frac[c], 1.0), -2.0 * math.pi, math.pi / 2)
 
         def lower_sin(c):
             sine(sin[c], frac[c], -2.0 * math.pi)
 
         def whole_turns_vector(c):
             n = work.tile([P, S], I32, name="turns_v", bufs=2)
-            nc.vector.tensor_scalar(out=n[:], in0=pos[:], scalar1=col(turn, c), scalar2=None, op0=ALU.mult)
+            nc.vector.tensor_scalar(out=n[:], in0=posg[:], scalar1=turn(c), scalar2=None, op0=ALU.mult)
             turns[c] = n[:]
 
         def whole_turns_scalar(c):
             n = work.tile([P, S], U32, name="turns_s", bufs=2)
-            nc.scalar.activation(out=n[:], in_=pos[:], func=ACT.Copy, scale=col(turn, c))
+            nc.scalar.activation(out=n[:], in_=posg[:], func=ACT.Copy, scale=turn(c))
             turns[c] = n[:].bitcast(I32)
 
         def fraction(c):
             frac[c] = keep.tile([P, S], F32, name="frac%d" % c)
             nc.vector.scalar_tensor_tensor(
-                out=frac[c][:], in0=pos[:], scalar=col(turn, c), in1=turns[c], op0=ALU.mult, op1=ALU.subtract
+                out=frac[c][:], in0=posg[:], scalar=turn(c), in1=turns[c], op0=ALU.mult, op1=ALU.subtract
             )
 
         units = [(m, c, b) for group in GROUPS for m in range(2) for b in range(NSEQ) for c in group]
@@ -242,7 +234,7 @@ def tile_ropemultiheadattention_pa_kernel(
 
         def w_codes(m, c, h, g):
             if c == FIRST:
-                return wc_first[m][:, g, h, :]
+                return wc_first[m][h][:, g, :]
             return wc_rest[m][:, g, h, 2 * P * c : 2 * P * (c + 1)]
 
         last_kind = ["mx"]

@@ -27,9 +27,11 @@ FIRST_DIRECT = 7
 PAIR_ORDER = (5, 4, 3, 2, 1, 0)
 FIRST = PAIR_ORDER[0]
 GROUPS = ((5,), (4,), (3,), (2,), (1, 0))
-TABLES_BEFORE = {1: (("lower", 4),), 3: (("lower", 3), ("turns", 2), ("turns", 1)), 5: (("lower", 2), ("turns", 0)), 6: (("lower", 1),), 7: (("lower", 0),)}
-TABLES_AFTER = {0: (("upper", 4), ("upper", 3)), 1: (("upper", 2), ("upper", 1)), 2: (("upper", 0),)}
-FRACTION_BEHIND = {4: 2, 5: 1, 6: 0}
+TABLES_BEFORE = {1: (("folds", 4), ("upper", 3), ("lower", 3)), 6: (("lower", 1),), 7: (("lower", 0),)}
+HEAD_BLOCKS = (5, 3, 2)
+FOLD_AT = (4.0 * math.pi, 2.0 * math.pi, math.pi)
+TABLES_AFTER = {0: (("upper", 4),), 2: (("upper", 2), ("turns", 1)), 3: (("lower", 2),), 4: (("upper", 1), ("turns", 0)), 5: (("upper", 0),)}
+FRACTION_BEHIND = {5: 1, 6: 0}
 ACC_SLOTS = (0, 0, 0, 0, 0, 0, 0, 0, 0, 0, 2, 4)
 WARM_MATMULS = 8
 BRIDGE_MATMULS = 4
@@ -206,6 +208,16 @@ def tile_ropemultiheadattention_pa_kernel(
             else:
                 sine(sin[c], fold(posg, frad(c), -math.pi / 2), -1.0, math.pi / 2)
 
+        def folded(c, shift):
+            a = fold(posg, frad(c), shift - FOLD_AT[0])
+            for at in FOLD_AT[1:]:
+                a = fold(a, 1.0, -at)
+            return a
+
+        def lower_by_folds(c):
+            sine(sin[c], folded(c, math.pi / 2), 1.0, -math.pi / 2)
+            sine(cos[c], folded(c, 0.0), 1.0, -math.pi / 2)
+
         def lower_cos(c):
             sine(cos[c], fold(frac[c], 1.0), -2.0 * math.pi, math.pi / 2)
 
@@ -377,11 +389,11 @@ def tile_ropemultiheadattention_pa_kernel(
                         nc.scalar.copy(out=flat_st, in_=tr[h, j][:, 0 : 2 * P])
                     store(u, h, 2 * j, st)
 
-        whole_turns_vector(PAIR_ORDER[0])
+        whole_turns_vector(HEAD_BLOCKS[0])
         for i in range(HEAD_FRACTIONS):
             if i + 1 < HEAD_FRACTIONS:
-                whole_turns_vector(PAIR_ORDER[i + 1])
-            fraction(PAIR_ORDER[i])
+                whole_turns_vector(HEAD_BLOCKS[i + 1])
+            fraction(HEAD_BLOCKS[i])
         upper_cos(FIRST + NPAIR)
         upper_sin(FIRST + NPAIR)
         lower_sin(FIRST)
@@ -400,6 +412,8 @@ def tile_ropemultiheadattention_pa_kernel(
                 elif kind == "lower":
                     lower_sin(c)
                     lower_cos(c)
+                elif kind == "folds":
+                    lower_by_folds(c)
                 else:
                     whole_turns_scalar(c)
 

@@ -33,8 +33,8 @@ FOLD_AT = (4.0 * math.pi, 2.0 * math.pi, math.pi)
 TABLES_AFTER = {0: (("upper", 4),), 2: (("upper", 2), ("turns", 1)), 3: (("lower", 2),), 4: (("upper", 1), ("turns", 0)), 5: (("upper", 0),)}
 FRACTION_BEHIND = {5: 1, 6: 0}
 ACC_SLOTS = (0, 0, 0, 0, 0, 0, 0, 0, 0, 0, 2, 4)
-WARM_MATMULS = 8
-BRIDGE_MATMULS = 4
+WARM_MATMULS = 6
+BRIDGE_MATMULS = 2
 SPACER_COLUMNS = 64
 HEAD_FRACTIONS = 3
 EARLY_STEPS = 2
@@ -96,7 +96,6 @@ def tile_ropemultiheadattention_pa_kernel(
         brows = keep.tile([P, BIAS_ROW], BF16, name="brows")
         nc.vector.memset(brows[:], 0.0)
         nc.vector.memset(warm[:], 0.0)
-        nc.vector.memset(flat(xs[0]).bitcast(I32), 0)
         nc.vector.memset(flat(ws[0]).bitcast(I32), 0)
 
         load_first_codes(0, 1)
@@ -104,6 +103,7 @@ def tile_ropemultiheadattention_pa_kernel(
             nc.scalar.dma_start(out=brows[4 * m : 4 * m + 4, :], in_=biases[m].rearrange("(r n) -> r n", n=BIAS_ROW))
         nc.scalar.activation(out=warm_out[:], in_=warm[:], func=ACT.Sin)
 
+        nc.gpsimd.memset(flat(xs[0]).bitcast(F32), 0.0)
         idx = keep.tile([P, 1], I32, name="idx")
         nc.gpsimd.iota(idx[:], pattern=[[1, 1]], base=P - 1, channel_multiplier=-1)
         zeros = keep.tile([P, S], BF16, name="zeros")

@@ -80,11 +80,11 @@ def tile_ropemultiheadattention_pa_kernel(
 
         def load_planes(dst, scales, first_col):
             ncols = dst.shape[2]
-            for q in range(4):
+            for r in range(4):
                 nc.sync.dma_start(
-                    out=dst[32 * q : 32 * q + 4, :, :].bitcast(I32),
-                    in_=scales[:, 4 * q : 4 * q + 4, first_col : first_col + ncols]
-                    .rearrange("g r n -> r g n")
+                    out=dst[r : P : 32, :, :].bitcast(I32),
+                    in_=scales[:, r : 16 : 4, first_col : first_col + ncols]
+                    .rearrange("g q n -> q g n")
                     .bitcast(I32),
                 )
 

@@ -37,7 +37,7 @@ WARM_MATMULS = 6
 BRIDGE_MATMULS = 2
 SPACER_COLUMNS = 64
 HEAD_FRACTIONS = 3
-EARLY_STEPS = 2
+UNIT_ADDS = (0, 1, 2, 3, 4, 7, 8, 9, 10)
 FLOPS = 2 * NSEQ * S * D * 2 * E
 
 
@@ -309,16 +309,17 @@ def tile_ropemultiheadattention_pa_kernel(
                 products(u, project(u), x, i)
                 if i == 0 and between is not None:
                     between()
-                if k < EARLY_STEPS:
+                if k in UNIT_ADDS and 2 * i < n_sum:
+                    top = min(2 * i + 2, n_sum)
                     nc.gpsimd.tensor_tensor(
-                        out=ow[:, 2 * i : 2 * i + 2, :],
-                        in0=x[:, 0, 2 * i : 2 * i + 2, :],
-                        in1=x[:, 1, 2 * i : 2 * i + 2, :],
+                        out=ow[:, 2 * i : top, :],
+                        in0=x[:, 0, 2 * i : top, :],
+                        in1=x[:, 1, 2 * i : top, :],
                         op=ALU.add,
                     )
             if hook is not None:
                 hook()
-            if n_sum > 0 and k >= EARLY_STEPS:
+            if n_sum > 0 and k not in UNIT_ADDS:
                 nc.gpsimd.tensor_tensor(out=ow[:], in0=x[:, 0, 0:n_sum, :], in1=x[:, 1, 0:n_sum, :], op=ALU.add)
 
         def turn_round(dst, u, h, t):

@@ -22,7 +22,6 @@ NBLK = E // P
 NPAIR = NBLK // 2
 NT = S // P
 BIAS_ROW = 3 * P
-FREQ_BITS = 6
 FIRST_DIRECT = 7
 PAIR_ORDER = (5, 4, 3, 2, 1, 0)
 FIRST = PAIR_ORDER[0]
@@ -94,25 +93,35 @@ def tile_ropemultiheadattention_pa_kernel(
         warm = keep.tile([P, 1], F32, name="warm")
         warm_out = keep.tile([P, 1], F32, name="warm_out")
         brows = keep.tile([P, BIAS_ROW], BF16, name="brows")
+        base = keep.tile([P, 1], F32, name="base")
+        idx = keep.tile([P, 1], I32, name="idx")
+        half = keep.tile([P, 1], I32, name="half")
+        expo = keep.tile([P, 1], F32, name="expo")
+        gfac = keep.tile([P, 1], F32, name="gfac")
+        nc.gpsimd.memset(flat(xs[0]).bitcast(F32), 0.0)
+        nc.gpsimd.iota(idx[:], pattern=[[1, 1]], base=0, channel_multiplier=1)
         nc.vector.memset(brows[:], 0.0)
         nc.vector.memset(warm[:], 0.0)
         nc.vector.memset(flat(ws[0]).bitcast(I32), 0)
+        nc.vector.memset(base[:], ROPE_BASE)
+        nc.vector.tensor_scalar(
+            out=half[:], in0=idx[:], scalar1=1, scalar2=P - 1, op0=ALU.logical_shift_right, op1=ALU.bitwise_and
+        )
+        nc.vector.tensor_scalar(out=expo[:], in0=half[:], scalar1=-1.0 / HALF, scalar2=0.0, op0=ALU.mult, op1=ALU.add)
+        nc.vector.memset(flat(xs[1]).bitcast(I32), 0)
 
         load_first_codes(0, 1)
         for m in range(2):
             nc.scalar.dma_start(out=brows[4 * m : 4 * m + 4, :], in_=biases[m].rearrange("(r n) -> r n", n=BIAS_ROW))
         nc.scalar.activation(out=warm_out[:], in_=warm[:], func=ACT.Sin)
 
-        nc.gpsimd.memset(flat(xs[0]).bitcast(F32), 0.0)
-        idx = keep.tile([P, 1], I32, name="idx")
-        nc.gpsimd.iota(idx[:], pattern=[[1, 1]], base=P - 1, channel_multiplier=-1)
         zeros = keep.tile([P, S], BF16, name="zeros")
         nc.gpsimd.memset(zeros[:], 0.0)
         pos = keep.tile([P, S], F32, name="pos")
         nc.gpsimd.iota(pos[:], pattern=[[1, S]], base=0, channel_multiplier=0, allow_small_or_imprecise_dtypes=True)
+        nc.gpsimd.tensor_tensor(out=gfac[:], in0=base[:], in1=expo[:], op=ALU.pow)
         ident = keep.tile([P, P], F32, name="ident")
         make_identity(nc, ident[:])
-        nc.gpsimd.memset(flat(xs[1]).bitcast(F32), 0.0)
         nc.gpsimd.memset(flat(ws[1]).bitcast(F32), 0.0)
 
         load_planes(xs[0], x_scales, 0)
@@ -132,42 +141,11 @@ def tile_ropemultiheadattention_pa_kernel(
         for i in range(WARM_MATMULS):
             nc.tensor.matmul(out=idle_ps[:], lhsT=zeros[:, 0:P], rhs=zeros[:], start=True, stop=True)
 
-        brows32 = keep.tile([P, BIAS_ROW], F32, name="brows32")
-        nc.scalar.copy(out=brows32[:], in_=brows[:])
-        bias_ps = psum.tile([P, S], F32, name="bank")
-        for j in range(3):
-            nc.tensor.transpose(
-                out=bias_ps[:, P * j : P * (j + 1)], in_=brows32[:, P * j : P * (j + 1)], identity=ident[:]
-            )
-        for i in range(BRIDGE_MATMULS):
-            nc.tensor.matmul(out=idle_ps[:], lhsT=zeros[:, 0:P], rhs=zeros[:], start=True, stop=True)
         bias = keep.tile([P, 3, 8], F32, name="bias")
-        nc.scalar.copy(out=bias[:], in_=bias_ps[:, 0:BIAS_ROW].rearrange("p (j r) -> p j r", j=3)[:, :, 0:8])
 
         def bias_col(m, blk):
             return bias[:, blk % 3, 4 * m + blk // 3 : 4 * m + blk // 3 + 1]
 
-        bit = keep.tile([P, FREQ_BITS], I32, name="bit")
-        fac = keep.tile([P, FREQ_BITS], F32, name="fac")
-        for k in range(FREQ_BITS):
-            nc.vector.tensor_scalar(
-                out=bit[:, k : k + 1], in0=idx[:], scalar1=k + 1, scalar2=1,
-                op0=ALU.logical_shift_right, op1=ALU.bitwise_and,
-            )
-        for k in range(FREQ_BITS):
-            nc.vector.tensor_scalar(
-                out=fac[:, k : k + 1], in0=bit[:, k : k + 1], scalar1=ROPE_BASE ** ((2.0 ** k) / HALF) - 1.0, scalar2=1.0,
-                op0=ALU.mult, op1=ALU.add,
-            )
-        p3 = keep.tile([P, 3], F32, name="p3")
-        p1 = keep.tile([P, 1], F32, name="p1")
-        gfac = keep.tile([P, 1], F32, name="gfac")
-        nc.vector.tensor_tensor(out=p3[:], in0=fac[:, 0:3], in1=fac[:, 3:6], op=ALU.mult)
-        nc.vector.tensor_tensor(out=p1[:], in0=p3[:, 0:1], in1=p3[:, 1:2], op=ALU.mult)
-        lowest = ROPE_BASE ** (-(2.0 ** FREQ_BITS - 1.0) / HALF)
-        nc.vector.scalar_tensor_tensor(
-            out=gfac[:], in0=p1[:], scalar=lowest, in1=p3[:, 2:3], op0=ALU.mult, op1=ALU.mult
-        )
         posg = keep.tile([P, S], F32, name="posg")
         nc.vector.tensor_scalar(out=posg[:], in0=pos[:], scalar1=gfac[:, 0:1], scalar2=None, op0=ALU.mult)
 
@@ -395,8 +373,18 @@ def tile_ropemultiheadattention_pa_kernel(
             if i + 1 < HEAD_FRACTIONS:
                 whole_turns_vector(HEAD_BLOCKS[i + 1])
             fraction(HEAD_BLOCKS[i])
+        brows32 = keep.tile([P, BIAS_ROW], F32, name="brows32")
+        nc.scalar.copy(out=brows32[:], in_=brows[:])
+        bias_ps = psum.tile([P, S], F32, name="bank")
+        for j in range(3):
+            nc.tensor.transpose(
+                out=bias_ps[:, P * j : P * (j + 1)], in_=brows32[:, P * j : P * (j + 1)], identity=ident[:]
+            )
+        for i in range(BRIDGE_MATMULS):
+            nc.tensor.matmul(out=idle_ps[:], lhsT=zeros[:, 0:P], rhs=zeros[:], start=True, stop=True)
         upper_cos(FIRST + NPAIR)
         upper_sin(FIRST + NPAIR)
+        nc.scalar.copy(out=bias[:], in_=bias_ps[:, 0:BIAS_ROW].rearrange("p (j r) -> p j r", j=3)[:, :, 0:8])
         lower_sin(FIRST)
         lower_cos(FIRST)
 

@@ -25,7 +25,7 @@ BIAS_ROW = 3 * P
 FIRST_DIRECT = 7
 PAIR_ORDER = (5, 4, 3, 2, 1, 0)
 FIRST = PAIR_ORDER[0]
-GROUPS = ((5,), (4,), (3,), (2,), (1, 0))
+GROUPS = ((5,), (4,), (3, 2), (1, 0))
 TABLES_BEFORE = {1: (("folds", 4), ("upper", 3), ("lower", 3)), 6: (("lower", 1),), 7: (("lower", 0),)}
 HEAD_BLOCKS = (5, 3, 2)
 FOLD_AT = (4.0 * math.pi, 2.0 * math.pi, math.pi)

@@ -36,7 +36,7 @@ WARM_MATMULS = 6
 BRIDGE_MATMULS = 2
 SPACER_COLUMNS = 64
 HEAD_FRACTIONS = 3
-UNIT_ADDS = (0, 1, 2, 3, 4, 7, 8, 9, 10)
+UNIT_ADDS = (0, 1, 2, 3, 4, 10)
 FLOPS = 2 * NSEQ * S * D * 2 * E
 
 

@@ -7,7 +7,6 @@ from concourse.masks import make_identity
 F32 = mybir.dt.float32
 BF16 = mybir.dt.bfloat16
 I32 = mybir.dt.int32
-U32 = mybir.dt.uint32
 U8 = mybir.dt.uint8
 FP4X4 = mybir.dt.float4_e2m1fn_x4
 ALU = mybir.AluOpType
@@ -29,7 +28,8 @@ GROUPS = ((5,), (4,), (3, 2), (1, 0))
 TABLES_BEFORE = {1: (("folds", 4), ("upper", 3), ("lower", 3)), 6: (("lower", 1),), 7: (("lower", 0),)}
 HEAD_BLOCKS = (5, 3, 2)
 FOLD_AT = (4.0 * math.pi, 2.0 * math.pi, math.pi)
-TABLES_AFTER = {0: (("upper", 4),), 2: (("upper", 2), ("turns", 1)), 3: (("lower", 2),), 4: (("upper", 1), ("turns", 0)), 5: (("upper", 0),)}
+TABLES_AFTER = {0: (("upper", 4),), 2: (("upper", 2),), 3: (("lower", 2),), 4: (("upper", 1),), 5: (("upper", 0),)}
+LOOP_BLOCKS = (1, 0)
 FRACTION_BEHIND = {5: 1, 6: 0}
 ACC_SLOTS = (0, 0, 0, 0, 0, 0, 0, 0, 0, 0, 2, 4)
 WARM_MATMULS = 6
@@ -207,10 +207,10 @@ def tile_ropemultiheadattention_pa_kernel(
             nc.vector.tensor_scalar(out=n[:], in0=posg[:], scalar1=turn(c), scalar2=None, op0=ALU.mult)
             turns[c] = n[:]
 
-        def whole_turns_scalar(c):
-            n = work.tile([P, S], U32, name="turns_s", bufs=2)
-            nc.scalar.activation(out=n[:], in_=posg[:], func=ACT.Copy, scale=turn(c))
-            turns[c] = n[:].bitcast(I32)
+        def whole_turns_gpsimd(c):
+            n = work.tile([P, S], I32, name="turns_v", bufs=2)
+            nc.gpsimd.tensor_scalar(out=n[:], in0=posg[:], scalar1=turn(c), scalar2=0.0, op0=ALU.mult, op1=ALU.add)
+            turns[c] = n[:]
 
         def fraction(c):
             frac[c] = keep.tile([P, S], F32, name="frac%d" % c)
@@ -373,6 +373,8 @@ def tile_ropemultiheadattention_pa_kernel(
             if i + 1 < HEAD_FRACTIONS:
                 whole_turns_vector(HEAD_BLOCKS[i + 1])
             fraction(HEAD_BLOCKS[i])
+        for c in LOOP_BLOCKS:
+            whole_turns_gpsimd(c)
         brows32 = keep.tile([P, BIAS_ROW], F32, name="brows32")
         nc.scalar.copy(out=brows32[:], in_=brows[:])
         bias_ps = psum.tile([P, S], F32, name="bank")
@@ -401,10 +403,8 @@ def tile_ropemultiheadattention_pa_kernel(
                 elif kind == "lower":
                     lower_sin(c)
                     lower_cos(c)
-                elif kind == "folds":
-                    lower_by_folds(c)
                 else:
-                    whole_turns_scalar(c)
+                    lower_by_folds(c)
 
         def emit_step(k):
             if joined[k]:

from contextlib import ExitStack
import math

import concourse.mybir as mybir
from concourse.masks import make_identity

F32 = mybir.dt.float32
BF16 = mybir.dt.bfloat16
I32 = mybir.dt.int32
U8 = mybir.dt.uint8
FP4X4 = mybir.dt.float4_e2m1fn_x4
ALU = mybir.AluOpType
ACT = mybir.ActivationFunctionType

NSEQ, S, D, E = 2, 512, 1536, 1536
ROPE_BASE = 10000.0
P = 128
PASSES = D // 512
HALF = E // 2
NBLK = E // P
NPAIR = NBLK // 2
NT = S // P
BIAS_ROW = 3 * P
FIRST_DIRECT = 7
PAIR_ORDER = (5, 4, 3, 2, 1, 0)
FIRST = PAIR_ORDER[0]
GROUPS = ((5,), (4,), (3, 2), (1, 0))
TABLES_BEFORE = {1: (("folds", 4), ("upper", 3), ("lower", 3)), 6: (("lower", 1),), 7: (("lower", 0),)}
HEAD_BLOCKS = (5, 3, 2)
FOLD_AT = (4.0 * math.pi, 2.0 * math.pi, math.pi)
TABLES_AFTER = {0: (("upper", 4),), 2: (("upper", 2),), 3: (("lower", 2),), 4: (("upper", 1),), 5: (("upper", 0),)}
LOOP_BLOCKS = (1, 0)
FRACTION_BEHIND = {5: 1, 6: 0}
ACC_SLOTS = (0, 0, 0, 0, 0, 0, 0, 0, 0, 0, 2, 4)
WARM_MATMULS = 6
BRIDGE_MATMULS = 2
SPACER_COLUMNS = 64
HEAD_FRACTIONS = 3
UNIT_ADDS = (0, 1, 2, 3, 4, 10)
FLOPS = 2 * NSEQ * S * D * 2 * E


def tile_ropemultiheadattention_pa_kernel(
    tc, x_words, x_scales, Wq_words, Wq_scales, bq, Wk_words, Wk_scales, bk, out_0, out_1
):
    nc = tc.nc
    w_words = (Wq_words, Wk_words)
    w_scales = (Wq_scales, Wk_scales)
    biases = (bq, bk)
    outs = (out_0, out_1)

    with ExitStack() as ctx:
        keep = ctx.enter_context(tc.tile_pool(name="keep", bufs=1))
        work = ctx.enter_context(tc.tile_pool(name="work", bufs=2))
        far = ctx.enter_context(tc.tile_pool(name="far", bufs=1))
        psum = ctx.enter_context(tc.psum_pool(name="psum", bufs=8))
        ctx.enter_context(tc.manual_schedule())

        xw = [far.tile([P, PASSES, 2 * S], U8, name="xw%d" % b, align_bytes=64) for b in range(NSEQ)]
        xs = [far.tile([P, PASSES, S], U8, name="xs%d" % b, align_bytes=64) for b in range(NSEQ)]
        ws = [keep.tile([P, PASSES, E], U8, name="ws%d" % m, align_bytes=64) for m in range(2)]
        wc_first = [
            [keep.tile([P, PASSES, 2 * P], U8, name="wcf%d_%d" % (m, h), align_bytes=64) for h in range(2)]
            for m in range(2)
        ]
        wc_rest = [
            keep.tile([P, PASSES, 2, 2 * P * FIRST], U8, name="wcr%d" % m, align_bytes=64) for m in range(2)
        ]

        def flat(t):
            return t[:].rearrange("p g n -> p (g n)")

        def load_codes(dst, words, first_byte):
            nbytes = dst.shape[2]
            nc.sync.dma_start(
                out=dst.bitcast(I32),
                in_=words[:, :, first_byte : first_byte + nbytes].rearrange("g p n -> p g n").bitcast(I32),
            )

        def load_planes(dst, scales, first_col):
            ncols = dst.shape[2]
            for r in range(4):
                nc.sync.dma_start(
                    out=dst[r : P : 32, :, :].bitcast(I32),
                    in_=scales[:, r : 16 : 4, first_col : first_col + ncols]
                    .rearrange("g q n -> q g n")
                    .bitcast(I32),
                )

        def load_first_codes(m, h):
            load_codes(wc_first[m][h][:, :, :], w_words[m], 2 * P * (FIRST + NPAIR * h))

        warm = keep.tile([P, 1], F32, name="warm")
        warm_out = keep.tile([P, 1], F32, name="warm_out")
        brows = keep.tile([P, BIAS_ROW], BF16, name="brows")
        base = keep.tile([P, 1], F32, name="base")
        idx = keep.tile([P, 1], I32, name="idx")
        half = keep.tile([P, 1], I32, name="half")
        expo = keep.tile([P, 1], F32, name="expo")
        gfac = keep.tile([P, 1], F32, name="gfac")
        nc.gpsimd.memset(flat(xs[0]).bitcast(F32), 0.0)
        nc.gpsimd.iota(idx[:], pattern=[[1, 1]], base=0, channel_multiplier=1)
        nc.vector.memset(brows[:], 0.0)
        nc.vector.memset(warm[:], 0.0)
        nc.vector.memset(flat(ws[0]).bitcast(I32), 0)
        nc.vector.memset(base[:], ROPE_BASE)
        nc.vector.tensor_scalar(
            out=half[:], in0=idx[:], scalar1=1, scalar2=P - 1, op0=ALU.logical_shift_right, op1=ALU.bitwise_and
        )
        nc.vector.tensor_scalar(out=expo[:], in0=half[:], scalar1=-1.0 / HALF, scalar2=0.0, op0=ALU.mult, op1=ALU.add)
        nc.vector.memset(flat(xs[1]).bitcast(I32), 0)

        load_first_codes(0, 1)
        for m in range(2):
            nc.scalar.dma_start(out=brows[4 * m : 4 * m + 4, :], in_=biases[m].rearrange("(r n) -> r n", n=BIAS_ROW))
        nc.scalar.activation(out=warm_out[:], in_=warm[:], func=ACT.Sin)

        zeros = keep.tile([P, S], BF16, name="zeros")
        nc.gpsimd.memset(zeros[:], 0.0)
        pos = keep.tile([P, S], F32, name="pos")
        nc.gpsimd.iota(pos[:], pattern=[[1, S]], base=0, channel_multiplier=0, allow_small_or_imprecise_dtypes=True)
        nc.gpsimd.tensor_tensor(out=gfac[:], in0=base[:], in1=expo[:], op=ALU.pow)
        ident = keep.tile([P, P], F32, name="ident")
        make_identity(nc, ident[:])
        nc.gpsimd.memset(flat(ws[1]).bitcast(F32), 0.0)

        load_planes(xs[0], x_scales, 0)
        load_codes(xw[0][:, :, :], x_words, 0)
        load_planes(ws[0], w_scales[0], 0)
        load_first_codes(0, 0)
        load_planes(xs[1], x_scales, S)
        load_codes(xw[1][:, :, :], x_words, 2 * S)
        load_planes(ws[1], w_scales[1], 0)
        load_first_codes(1, 1)
        load_first_codes(1, 0)
        for m in range(2):
            for h in (1, 0):
                load_codes(wc_rest[m][:, :, h, :], w_words[m], 2 * HALF * h)

        idle_ps = psum.tile([P, S], F32, name="bank")
        for i in range(WARM_MATMULS):
            nc.tensor.matmul(out=idle_ps[:], lhsT=zeros[:, 0:P], rhs=zeros[:], start=True, stop=True)

        bias = keep.tile([P, 3, 8], F32, name="bias")

        def bias_col(m, blk):
            return bias[:, blk % 3, 4 * m + blk // 3 : 4 * m + blk // 3 + 1]

        posg = keep.tile([P, S], F32, name="posg")
        nc.vector.tensor_scalar(out=posg[:], in0=pos[:], scalar1=gfac[:, 0:1], scalar2=None, op0=ALU.mult)

        def frad(c):
            return ROPE_BASE ** (-c / float(NBLK))

        def turn(c):
            return frad(c) * 0.5 / math.pi

        tabs = [[keep.tile([P, 2, S], F32, name="tab%d_%d" % (c, s)) for s in range(2)] for c in range(NPAIR)]
        cos = {}
        sin = {}
        for c in range(NPAIR):
            cos[c] = tabs[c][0][:, 0, :]
            sin[c + NPAIR] = tabs[c][0][:, 1, :]
            sin[c] = tabs[c][1][:, 0, :]
            cos[c + NPAIR] = tabs[c][1][:, 1, :]
        turns = {}
        frac = {}

        def sine(out, in_, scale, bias=0.0):
            nc.scalar.activation(out=out, in_=in_[:], func=ACT.Sin, scale=scale, bias=bias)

        def fold(in_, scale, bias=0.0):
            a = work.tile([P, S], F32, name="folded")
            nc.scalar.activation(out=a[:], in_=in_[:], func=ACT.Abs, scale=scale, bias=bias)
            return a

        def upper_cos(c):
            if c >= FIRST_DIRECT:
                sine(cos[c], posg, -frad(c), math.pi / 2)
            else:
                sine(cos[c], fold(posg, frad(c), -math.pi), 1.0, -math.pi / 2)

        def upper_sin(c):
            if c >= FIRST_DIRECT:
                sine(sin[c], posg, frad(c))
            else:
                sine(sin[c], fold(posg, frad(c), -math.pi / 2), -1.0, math.pi / 2)

        def folded(c, shift):
            a = fold(posg, frad(c), shift - FOLD_AT[0])
            for at in FOLD_AT[1:]:
                a = fold(a, 1.0, -at)
            return a

        def lower_by_folds(c):
            sine(sin[c], folded(c, math.pi / 2), 1.0, -math.pi / 2)
            sine(cos[c], folded(c, 0.0), 1.0, -math.pi / 2)

        def lower_cos(c):
            sine(cos[c], fold(frac[c], 1.0), -2.0 * math.pi, math.pi / 2)

        def lower_sin(c):
            sine(sin[c], frac[c], -2.0 * math.pi)

        def whole_turns_vector(c):
            n = work.tile([P, S], I32, name="turns_v", bufs=2)
            nc.vector.tensor_scalar(out=n[:], in0=posg[:], scalar1=turn(c), scalar2=None, op0=ALU.mult)
            turns[c] = n[:]

        def whole_turns_gpsimd(c):
            n = work.tile([P, S], I32, name="turns_v", bufs=2)
            nc.gpsimd.tensor_scalar(out=n[:], in0=posg[:], scalar1=turn(c), scalar2=0.0, op0=ALU.mult, op1=ALU.add)
            turns[c] = n[:]

        def fraction(c):
            frac[c] = keep.tile([P, S], F32, name="frac%d" % c)
            nc.vector.scalar_tensor_tensor(
                out=frac[c][:], in0=posg[:], scalar=turn(c), in1=turns[c], op0=ALU.mult, op1=ALU.subtract
            )

        units = [(m, c, b) for group in GROUPS for m in range(2) for b in range(NSEQ) for c in group]
        joined = [len(group) == 2 for group in GROUPS for i in range(2 * len(group))]
        last = len(units) - 1

        def w_codes(m, c, h, g):
            if c == FIRST:
                return wc_first[m][h][:, g, :]
            return wc_rest[m][:, g, h, 2 * P * c : 2 * P * (c + 1)]

        last_kind = ["mx"]

        def spacer(bank, kind):
            if last_kind[0] != kind:
                nc.tensor.matmul(
                    out=bank[:, 0:SPACER_COLUMNS], lhsT=zeros[:, 0:P], rhs=zeros[:, 0:SPACER_COLUMNS], start=True, stop=True
                )
            last_kind[0] = kind

        def project(u):
            m, c, b = units[u]
            bank_a = psum.tile([P, S], F32, name="bank")
            bank_b = psum.tile([P, S], F32, name="bank")
            spacer(bank_a, "mx")
            acc = {1: bank_a, 0: bank_b}
            for h in (1, 0):
                blk = c + NPAIR * h
                for g in range(PASSES):
                    nc.tensor.matmul_mx(
                        out=acc[h][:],
                        lhsT=w_codes(m, c, h, g).bitcast(FP4X4),
                        lhsT_scale=ws[m][:, g, P * blk : P * (blk + 1)],
                        rhs=xw[b][:, g, :].bitcast(FP4X4),
                        rhs_scale=xs[b][:, g, :],
                        start=(g == 0),
                        stop=(g == PASSES - 1),
                    )
            return acc

        def products(u, acc, x, i):
            m, c, b = units[u]
            for src in (1, 0):
                nc.vector.scalar_tensor_tensor(
                    out=x[:, src, 2 * i : 2 * i + 2, :],
                    in0=acc[src][:].unsqueeze(1).to_broadcast([P, 2, S]),
                    scalar=bias_col(m, c + NPAIR * src),
                    in1=tabs[c][src][:],
                    op0=ALU.add,
                    op1=ALU.mult,
                )

        rotated = {}

        def rotate_pair(k, hook, between):
            n_sum = 4 - ACC_SLOTS[k]
            x = work.tile([P, 2, 4, S], F32, name="x", bufs=3)
            if n_sum > 0:
                ow = work.tile([P, n_sum, S], F32, name="ow", bufs=3)
            for i in range(2):
                u = 2 * k + i
                rotated[u] = {}
                for h in (0, 1):
                    slot = 2 * i + h
                    if slot < n_sum:
                        rotated[u][h] = [ow[:, slot, :]]
                    else:
                        rotated[u][h] = [x[:, 0, slot, :], x[:, 1, slot, :]]
                products(u, project(u), x, i)
                if i == 0 and between is not None:
                    between()
                if k in UNIT_ADDS and 2 * i < n_sum:
                    top = min(2 * i + 2, n_sum)
                    nc.gpsimd.tensor_tensor(
                        out=ow[:, 2 * i : top, :],
                        in0=x[:, 0, 2 * i : top, :],
                        in1=x[:, 1, 2 * i : top, :],
                        op=ALU.add,
                    )
            if hook is not None:
                hook()
            if n_sum > 0 and k not in UNIT_ADDS:
                nc.gpsimd.tensor_tensor(out=ow[:], in0=x[:, 0, 0:n_sum, :], in1=x[:, 1, 0:n_sum, :], op=ALU.add)

        def turn_round(dst, u, h, t):
            parts = rotated[u][h]
            for i, part in enumerate(parts):
                nc.tensor.matmul(
                    out=dst,
                    lhsT=part[:, P * t : P * (t + 1)],
                    rhs=ident[:],
                    is_transpose=True,
                    start=(i == 0),
                    stop=(i == len(parts) - 1),
                )

        def store(u, h, t0, st):
            m, c, b = units[u]
            blk = c + NPAIR * h
            rows = outs[m][b].rearrange("(t p) e -> p t e", p=P)
            nc.sync.dma_start(out=rows[:, t0 : t0 + st.shape[1], P * blk : P * (blk + 1)], in_=st[:])

        def emit(batch):
            tr = {}
            for u in batch:
                for h in (1, 0):
                    tr[u, h] = psum.tile([P, S], F32, name="bank")
                    spacer(tr[u, h], "transpose")
                    for t in range(NT):
                        turn_round(tr[u, h][:, P * t : P * (t + 1)], u, h, t)
            for u in batch:
                for h in (1, 0):
                    st = work.tile([P, NT, P], F32, name="st", bufs=8)
                    nc.scalar.copy(out=st[:].rearrange("p t e -> p (t e)"), in_=tr[u, h][:])
                    store(u, h, 0, st)

        def emit_joined(k):
            m, c, b = units[2 * k + 1]
            rows = outs[m][b].rearrange("(t p) e -> p t e", p=P)
            tr = {}
            for h in (1, 0):
                for j in range(2):
                    tr[h, j] = psum.tile([P, S], F32, name="bank")
                    spacer(tr[h, j], "transpose")
                    for t in range(2):
                        for i in range(2):
                            turn_round(tr[h, j][:, P * (2 * t + i) : P * (2 * t + i + 1)], 2 * k + 1 - i, h, 2 * j + t)
            for h in (1, 0):
                blk = c + NPAIR * h
                for j in range(2):
                    st = work.tile([P, 2, 2 * P], F32, name="st", bufs=8)
                    nc.scalar.copy(out=st[:].rearrange("p t e -> p (t e)"), in_=tr[h, j][:])
                    nc.sync.dma_start(out=rows[:, 2 * j : 2 * j + 2, P * blk : P * (blk + 2)], in_=st[:])

        def emit_last(u):
            tr = {}
            for h in (1, 0):
                for j in range(2):
                    tr[h, j] = psum.tile([P, S], F32, name="bank")
                    spacer(tr[h, j], "transpose")
                    for t in range(2):
                        turn_round(tr[h, j][:, P * t : P * (t + 1)], u, h, 2 * j + t)
            for h in (1, 0):
                for j in range(2):
                    st = work.tile([P, 2, P], F32, name="st2", bufs=4)
                    flat_st = st[:].rearrange("p t e -> p (t e)")
                    if j == 1:
                        nc.vector.tensor_copy(out=flat_st, in_=tr[h, j][:, 0 : 2 * P])
                    else:
                        nc.scalar.copy(out=flat_st, in_=tr[h, j][:, 0 : 2 * P])
                    store(u, h, 2 * j, st)

        whole_turns_vector(HEAD_BLOCKS[0])
        for i in range(HEAD_FRACTIONS):
            if i + 1 < HEAD_FRACTIONS:
                whole_turns_vector(HEAD_BLOCKS[i + 1])
            fraction(HEAD_BLOCKS[i])
        for c in LOOP_BLOCKS:
            whole_turns_gpsimd(c)
        brows32 = keep.tile([P, BIAS_ROW], F32, name="brows32")
        nc.scalar.copy(out=brows32[:], in_=brows[:])
        bias_ps = psum.tile([P, S], F32, name="bank")
        for j in range(3):
            nc.tensor.transpose(
                out=bias_ps[:, P * j : P * (j + 1)], in_=brows32[:, P * j : P * (j + 1)], identity=ident[:]
            )
        for i in range(BRIDGE_MATMULS):
            nc.tensor.matmul(out=idle_ps[:], lhsT=zeros[:, 0:P], rhs=zeros[:], start=True, stop=True)
        upper_cos(FIRST + NPAIR)
        upper_sin(FIRST + NPAIR)
        nc.scalar.copy(out=bias[:], in_=bias_ps[:, 0:BIAS_ROW].rearrange("p (j r) -> p j r", j=3)[:, :, 0:8])
        lower_sin(FIRST)
        lower_cos(FIRST)

        def fraction_of(c):
            def run():
                fraction(c)
            return run

        def make_tables(jobs):
            for kind, c in jobs:
                if kind == "upper":
                    upper_cos(c + NPAIR)
                    upper_sin(c + NPAIR)
                elif kind == "lower":
                    lower_sin(c)
                    lower_cos(c)
                else:
                    lower_by_folds(c)

        def emit_step(k):
            if joined[k]:
                emit_joined(k)
            else:
                emit([2 * k, 2 * k + 1])

        def emit_step_of(k):
            def run():
                emit_step(k)
            return run

        npairs = len(units) // 2
        for k in range(npairs):
            make_tables(TABLES_BEFORE.get(k, ()))
            at_end = k == npairs - 1
            rotate_pair(
                k, fraction_of(FRACTION_BEHIND[k]) if k in FRACTION_BEHIND else None, emit_step_of(k - 2) if at_end else None
            )
            if k >= 2 and not at_end:
                emit_step(k - 2)
            make_tables(TABLES_AFTER.get(k, ()))
        emit_step(npairs - 2)
        emit([last - 1])
        emit_last(last)
